import numpy as np
import ml_dtypes


def mxq(x, axis, fmt="e4m3"):
    dtype, down = {"e4m3": (ml_dtypes.float8_e4m3fn, 7), "e5m2": (ml_dtypes.float8_e5m2, 14)}[fmt]
    v = np.moveaxis(np.asarray(x, np.float32).astype(ml_dtypes.bfloat16).astype(np.float64), axis, -1)
    blocks = v.reshape(v.shape[:-1] + (-1, 32))
    amax = np.abs(blocks).max(-1, keepdims=True)
    byte = np.maximum(np.where(amax > 0, np.frexp(amax)[1] - 1 + 127, 0) - down, 1)
    scale = np.exp2(byte - 127.0)
    codes = (blocks / scale).astype(np.float32).astype(dtype).astype(np.float64)
    return np.moveaxis((codes * scale).reshape(v.shape), -1, axis)


WIDE = False


def mx_kscale(k):
    if not WIDE:
        return np.ones(k)
    levels = np.array([10, -10, 5, -5, 0])
    a = np.random.permutation(np.resize(levels, k // 512 * 4)).reshape(k // 512, 4)
    idx = np.arange(k)
    return np.exp2(a[idx // 512, idx % 128 // 32])


BF16 = ml_dtypes.bfloat16


def bf(x):
    return np.asarray(x, np.float32).astype(BF16)


def f64(x):
    return np.asarray(x).astype(np.float64)


S, D, H, DH, F = 512, 1024, 8, 128, 4096
E = H * DH
EPS = 1e-5
XS = 0.015


def fixed_pos_embedding(seq_len, dim):
    inv_freq = 1.0 / (10000.0 ** (np.arange(0, dim, 2) / dim))
    sinusoid = np.arange(seq_len, dtype=np.float64)[:, None] * inv_freq[None, :]
    sin = np.concatenate([np.sin(sinusoid)] * 2, axis=-1)[:, :dim]
    cos = np.concatenate([np.cos(sinusoid)] * 2, axis=-1)[:, :dim]
    return sin, cos


def rotate_every_two(y):
    return np.stack((-y[..., 1::2], y[..., ::2]), axis=-1).reshape(y.shape)


def apply_rotary(y, sin, cos):
    return rotate_every_two(y) * sin[:, None, :] + y * cos[:, None, :]


def layernorm(x, scale, offset):
    mean = x.mean(axis=-1, keepdims=True)
    var = x.var(axis=-1, keepdims=True)
    return scale / np.sqrt(var + EPS) * (x - mean) + offset


def setup_inputs():
    s = mx_kscale(D)
    x = np.random.standard_normal((S, D)) + 0.5 * np.random.standard_normal(S)[:, None]
    return {"x": bf(XS * x[None]),
            "ln_scale": bf((1.0 + 0.1 * np.random.standard_normal(D)) * s),
            "ln_offset": bf(0.1 * np.random.standard_normal(D) * s),
            "Wq": bf(np.random.standard_normal((D, E)) * 0.7 / np.sqrt(D) / s[:, None]),
            "Wk": bf(np.random.standard_normal((D, E)) * 0.7 / np.sqrt(D) / s[:, None]),
            "Wv": bf(np.random.standard_normal((D, E)) / np.sqrt(D) / s[:, None])}


def reference(x, ln_scale, ln_offset, Wq, Wk, Wv):
    x = f64(x)
    b, s, _ = x.shape
    xn = layernorm(x, f64(ln_scale), f64(ln_offset))
    xq = mxq(xn, 2, "e4m3")

    def proj(W):
        h = (xq @ mxq(f64(W), 0, "e4m3")).reshape(b, s, H, DH)
        return np.transpose(h, (1, 0, 2, 3)).reshape(s, b * H, DH)

    q, v, k = proj(Wq), proj(Wv), proj(Wk)
    sin, cos = fixed_pos_embedding(s, DH)
    return apply_rotary(q, sin, cos), apply_rotary(k, sin, cos), v

@@ -1,0 +1,296 @@
+import math
+from contextlib import ExitStack
+
+import concourse.mybir as mybir
+from concourse.masks import make_identity
+
+F32 = mybir.dt.float32
+BF16 = mybir.dt.bfloat16
+U32 = mybir.dt.uint32
+U8 = mybir.dt.uint8
+FP8X4 = mybir.dt.float8_e4m3fn_x4
+ALU = mybir.AluOpType
+ACT = mybir.ActivationFunctionType
+
+P = 128
+TOKENS = 512
+D = 1024
+E = 1024
+PACK = 4
+K_PASS = P * PACK
+PASSES = D // K_PASS
+TOKEN_TILES = TOKENS // P
+CHUNK = 512
+CHUNKS = E // CHUNK
+ANGLES = 64
+REPEATS = CHUNK // ANGLES
+EPS = 1e-5
+BN_STATS_MAX = 512
+BN_STATS_DIM = 6
+
+FREQ_RATIO = 10000.0 ** (-1.0 / ANGLES)
+ROUND_MAGIC = 1.5 * 2.0**23
+TWO_PI_HIGH = 6.28125
+TWO_PI_LOW = 2.0 * math.pi - TWO_PI_HIGH
+
+FLOPS = 2 * TOKENS * D * 3 * E
+
+
+def tile_transformerlayershard_pa_kernel(
+    tc, x, ln_scale, ln_offset, Wq, Wk, Wv, out_0, out_1, out_2
+):
+    nc = tc.nc
+    weights = (Wq, Wk, Wv)
+    out_rows = [o.rearrange("s h d -> s (h d)") for o in (out_0, out_1, out_2)]
+    x_rows = x.rearrange("b s d -> (b s) d")
+
+    with ExitStack() as stack:
+        resident = stack.enter_context(tc.tile_pool(name="resident", bufs=1))
+        small = stack.enter_context(tc.tile_pool(name="small", bufs=4))
+        norm = stack.enter_context(tc.tile_pool(name="norm", bufs=2))
+        regroup = stack.enter_context(tc.tile_pool(name="regroup", bufs=4))
+        work = stack.enter_context(tc.tile_pool(name="work", bufs=3))
+        results = stack.enter_context(tc.tile_pool(name="results", bufs=6))
+        psum = stack.enter_context(tc.psum_pool(name="psum", bufs=8))
+
+        x_tiles = []
+        for tt in range(TOKEN_TILES):
+            x_tile = resident.tile([P, D], BF16, name="x_tile%d" % tt)
+            nc.sync.dma_start(out=x_tile[:], in_=x_rows[tt * P : (tt + 1) * P, :])
+            x_tiles.append(x_tile)
+
+        gain_bf = resident.tile([P, PASSES, PACK], BF16, name="gain_bf")
+        offset_bf = resident.tile([P, PASSES, PACK], BF16, name="offset_bf")
+        with nc.allow_non_contiguous_dma(reason="two vectors of 1024, four values to a piece"):
+            nc.scalar.dma_start(
+                out=gain_bf[:], in_=ln_scale.rearrange("(g p t) -> p g t", g=PASSES, t=PACK)
+            )
+            nc.scalar.dma_start(
+                out=offset_bf[:], in_=ln_offset.rearrange("(g p t) -> p g t", g=PASSES, t=PACK)
+            )
+
+        w_rows = {}
+        for m in range(3):
+            for g in range(PASSES):
+                w_tile = resident.tile([P, PACK, E], BF16, name="w_rows%d_%d" % (m, g))
+                nc.sync.dma_start(
+                    out=w_tile[:],
+                    in_=weights[m][g * K_PASS : (g + 1) * K_PASS, :].rearrange(
+                        "(p t) n -> p t n", t=PACK
+                    ),
+                )
+                w_rows[(m, g)] = w_tile
+
+        identity = resident.tile([P, P], F32, name="identity")
+        make_identity(nc, identity[:])
+        minus_half = resident.tile([P, 1], F32, name="minus_half")
+        nc.vector.memset(minus_half[:], -0.5)
+        gain = resident.tile([P, PASSES * PACK], F32, name="gain")
+        offset = resident.tile([P, PASSES * PACK], F32, name="offset")
+        nc.vector.tensor_copy(out=gain[:], in_=gain_bf[:].rearrange("p g t -> p (g t)"))
+        nc.vector.tensor_copy(out=offset[:], in_=offset_bf[:].rearrange("p g t -> p (g t)"))
+
+        position = resident.tile([P, TOKEN_TILES], F32, name="position")
+        nc.gpsimd.iota(
+            position[:],
+            pattern=[[P, TOKEN_TILES]],
+            base=0,
+            channel_multiplier=1,
+            allow_small_or_imprecise_dtypes=True,
+        )
+        signed_freq = resident.tile([P, ANGLES], F32, name="signed_freq")
+        nc.vector.memset(signed_freq[:, 0:1], -1.0)
+        for doubling in range(6):
+            width = 2**doubling
+            nc.vector.tensor_scalar_mul(
+                out=signed_freq[:, width : 2 * width],
+                in0=signed_freq[:, 0:width],
+                scalar1=(-FREQ_RATIO) ** width,
+            )
+        phase = resident.tile([P, 2, TOKEN_TILES, ANGLES], F32, name="phase")
+        turns = resident.tile([P, 2, TOKEN_TILES, ANGLES], F32, name="turns")
+        trig = resident.tile([P, 2, TOKEN_TILES, ANGLES], F32, name="trig")
+        phase_flat = phase[:].rearrange("p a b c -> p (a b c)")
+        turns_flat = turns[:].rearrange("p a b c -> p (a b c)")
+        for tt in range(TOKEN_TILES):
+            nc.vector.tensor_scalar_mul(
+                out=phase[:, 0, tt, :], in0=signed_freq[:], scalar1=position[:, tt : tt + 1]
+            )
+        nc.vector.tensor_scalar_add(
+            out=phase[:, 1].rearrange("p b c -> p (b c)"),
+            in0=phase[:, 0].rearrange("p b c -> p (b c)"),
+            scalar1=-0.5 * math.pi,
+        )
+        nc.vector.tensor_scalar(
+            out=turns_flat,
+            in0=phase_flat,
+            scalar1=0.5 / math.pi,
+            scalar2=ROUND_MAGIC,
+            op0=ALU.mult,
+            op1=ALU.add,
+        )
+        nc.vector.tensor_scalar_sub(out=turns_flat, in0=turns_flat, scalar1=ROUND_MAGIC)
+        for part_of_two_pi in (TWO_PI_HIGH, TWO_PI_LOW):
+            nc.vector.scalar_tensor_tensor(
+                out=phase_flat,
+                in0=turns_flat,
+                scalar=-part_of_two_pi,
+                in1=phase_flat,
+                op0=ALU.mult,
+                op1=ALU.add,
+            )
+        nc.vector.scalar_tensor_tensor(
+            out=turns_flat,
+            in0=phase_flat,
+            scalar=-1.0,
+            in1=phase_flat,
+            op0=ALU.mult,
+            op1=ALU.max,
+        )
+        nc.scalar.activation(
+            out=trig[:].rearrange("p a b c -> p (a b c)"),
+            in_=turns_flat,
+            func=ACT.Sin,
+            scale=-1.0,
+            bias=0.5 * math.pi,
+        )
+
+        x_codes = []
+        x_scales = []
+
+        def layer_norm_tile(tt):
+            x_tile = x_tiles[tt]
+            stats = small.tile([P, D // BN_STATS_MAX, BN_STATS_DIM], F32, name="stats")
+            for part in range(D // BN_STATS_MAX):
+                nc.vector.bn_stats(
+                    out=stats[:, part, :],
+                    in_=x_tile[:, part * BN_STATS_MAX : (part + 1) * BN_STATS_MAX],
+                )
+            mean_var = small.tile([P, 2], F32, name="mean_var")
+            nc.vector.bn_aggr(out=mean_var[:], in_=stats[:].rearrange("p a b -> p (a b)"))
+            var_eps = small.tile([P, 1], F32, name="var_eps")
+            nc.gpsimd.tensor_scalar_add(out=var_eps[:], in0=mean_var[:, 1:2], scalar1=EPS)
+            rstd = small.tile([P, 1], F32, name="rstd")
+            nc.gpsimd.tensor_tensor(out=rstd[:], in0=var_eps[:], in1=minus_half[:], op=ALU.pow)
+            shift = small.tile([P, 1], F32, name="shift")
+            nc.vector.scalar_tensor_tensor(
+                out=shift[:],
+                in0=mean_var[:, 0:1],
+                scalar=-1.0,
+                in1=rstd[:],
+                op0=ALU.mult,
+                op1=ALU.mult,
+            )
+            z = norm.tile([P, PASSES, PACK, P], F32, name="z")
+            nc.scalar.activation(
+                out=z[:],
+                in_=x_tile[:].rearrange("q (g c t) -> q g t c", g=PASSES, t=PACK),
+                func=ACT.Identity,
+                scale=rstd[:, 0:1],
+                bias=shift[:, 0:1],
+            )
+            planes = norm.tile([P, PASSES, PACK, P], BF16, name="planes")
+            for g in range(PASSES):
+                z_t = psum.tile([P, PACK, P], F32, name="z_t", tag="bank")
+                for t in range(PACK):
+                    nc.tensor.transpose(z_t[:, t, :], z[:, g, t, :], identity[:])
+                for t in range(PACK):
+                    nc.scalar.activation(
+                        out=planes[:, g, t, :],
+                        in_=z_t[:, t, :],
+                        func=ACT.Identity,
+                        scale=gain[:, g * PACK + t : g * PACK + t + 1],
+                        bias=offset[:, g * PACK + t : g * PACK + t + 1],
+                    )
+            grouped = norm.tile([P, PASSES, P, PACK], BF16, name="x_grouped", align_bytes=64)
+            nc.vector.tensor_copy(out=grouped[:], in_=planes[:].rearrange("p g t r -> p g r t"))
+            codes = resident.tile([P, PASSES, P], U32, name="x_codes%d" % tt, align_bytes=64)
+            scales = resident.tile([P, PASSES, P], U8, name="x_scales%d" % tt, align_bytes=64)
+            nc.vector.quantize_mx(
+                out=codes[:].rearrange("p g r -> p (g r)").bitcast(FP8X4),
+                scales=scales[:].rearrange("p g r -> p (g r)"),
+                in_=grouped[:].rearrange("p g r t -> p (g r t)"),
+            )
+            x_codes.append(codes)
+            x_scales.append(scales)
+
+        w_codes = {}
+        w_scales = {}
+
+        def quantise_weight_chunk(m, c, copy):
+            codes = resident.tile([P, PASSES, CHUNK], U32, name="w_codes%d_%d" % (m, c), align_bytes=64)
+            scales = resident.tile([P, PASSES, CHUNK], U8, name="w_scales%d_%d" % (m, c), align_bytes=64)
+            for g in range(PASSES):
+                grouped = regroup.tile([P, CHUNK, PACK], BF16, name="w_grouped", align_bytes=64)
+                copy(
+                    out=grouped[:].rearrange("p (a i) t -> p a t i", i=4),
+                    in_=w_rows[(m, g)][:, :, c * CHUNK : (c + 1) * CHUNK].rearrange(
+                        "p t (a i) -> p a t i", i=4
+                    ),
+                )
+                nc.vector.quantize_mx(
+                    out=codes[:, g, :].bitcast(FP8X4),
+                    scales=scales[:, g, :],
+                    in_=grouped[:].rearrange("p n t -> p (n t)"),
+                )
+            w_codes[(m, c)] = codes
+            w_scales[(m, c)] = scales
+
+        def rope(acc, tt, result):
+            straight = work.tile([P, CHUNK], F32, name="straight")
+            nc.vector.tensor_tensor(
+                out=straight[:].rearrange("p (r m) -> p r m", m=ANGLES),
+                in0=acc[:].rearrange("p (r m) -> p r m", m=ANGLES),
+                in1=trig[:, 0, tt, :].unsqueeze(1).to_broadcast([P, REPEATS, ANGLES]),
+                op=ALU.mult,
+            )
+            crossed = work.tile([P, 2, CHUNK // 2], F32, name="crossed")
+            y_pairs = acc[:].rearrange("p (r i two) -> p r i two", r=REPEATS, two=2)
+            sin_pairs = trig[:, 1, tt, :].rearrange("p (i two) -> p i two", two=2)
+            for parity in range(2):
+                nc.vector.tensor_tensor(
+                    out=crossed[:, parity, :].rearrange("p (r i) -> p r i", r=REPEATS),
+                    in0=y_pairs[:, :, :, 1 - parity],
+                    in1=sin_pairs[:, :, parity]
+                    .unsqueeze(1)
+                    .to_broadcast([P, REPEATS, ANGLES // 2]),
+                    op=ALU.mult,
+                )
+            nc.gpsimd.tensor_tensor(
+                out=result[:].rearrange("p (n two) -> p n two", two=2),
+                in0=straight[:].rearrange("p (n two) -> p n two", two=2),
+                in1=crossed[:].rearrange("p two n -> p n two"),
+                op=ALU.add,
+            )
+
+        def project_chunk(m, c):
+            for tt in range(TOKEN_TILES):
+                acc = psum.tile([P, CHUNK], F32, name="acc", tag="bank")
+                for g in range(PASSES):
+                    nc.tensor.matmul_mx(
+                        out=acc[:],
+                        lhsT=x_codes[tt][:, g, :].bitcast(FP8X4),
+                        lhsT_scale=x_scales[tt][:, g, :],
+                        rhs=w_codes[(m, c)][:, g, :].bitcast(FP8X4),
+                        rhs_scale=w_scales[(m, c)][:, g, :],
+                        start=(g == 0),
+                        stop=(g == PASSES - 1),
+                    )
+                result = results.tile([P, CHUNK], F32, name="result")
+                if m < 2:
+                    rope(acc, tt, result)
+                else:
+                    nc.scalar.copy(out=result[:], in_=acc[:])
+                nc.sync.dma_start(
+                    out=out_rows[m][tt * P : (tt + 1) * P, c * CHUNK : (c + 1) * CHUNK],
+                    in_=result[:],
+                )
+
+        for tt in range(TOKEN_TILES):
+            layer_norm_tile(tt)
+        chunks = [(m, c) for m in range(3) for c in range(CHUNKS)]
+        quantise_weight_chunk(0, 0, nc.vector.tensor_copy)
+        for index in range(len(chunks)):
+            if index + 1 < len(chunks):
+                quantise_weight_chunk(chunks[index + 1][0], chunks[index + 1][1], nc.scalar.copy)
+            project_chunk(chunks[index][0], chunks[index][1])

@@ -24,6 +24,7 @@ CHUNK = 512
 CHUNKS = E // CHUNK
 ANGLES = 64
 REPEATS = CHUNK // ANGLES
+RUN = 4
 EPS = 1e-5
 BN_STATS_MAX = 512
 BN_STATS_DIM = 6
@@ -32,6 +33,10 @@ FREQ_RATIO = 10000.0 ** (-1.0 / ANGLES)
 ROUND_MAGIC = 1.5 * 2.0**23
 TWO_PI_HIGH = 6.28125
 TWO_PI_LOW = 2.0 * math.pi - TWO_PI_HIGH
+PI_BELOW = 3.1415925
+
+LOOKAHEAD = 3
+QUANTISE_EVERY = 3
 
 FLOPS = 2 * TOKENS * D * 3 * E
 
@@ -43,15 +48,15 @@ def tile_transformerlayershard_pa_kernel(
     weights = (Wq, Wk, Wv)
     out_rows = [o.rearrange("s h d -> s (h d)") for o in (out_0, out_1, out_2)]
     x_rows = x.rearrange("b s d -> (b s) d")
+    chunks = [(m, c) for m in range(3) for c in range(CHUNKS)]
 
     with ExitStack() as stack:
+        stack.enter_context(tc.manual_schedule())
         resident = stack.enter_context(tc.tile_pool(name="resident", bufs=1))
         small = stack.enter_context(tc.tile_pool(name="small", bufs=4))
-        norm = stack.enter_context(tc.tile_pool(name="norm", bufs=2))
-        regroup = stack.enter_context(tc.tile_pool(name="regroup", bufs=4))
-        work = stack.enter_context(tc.tile_pool(name="work", bufs=3))
-        results = stack.enter_context(tc.tile_pool(name="results", bufs=6))
-        psum = stack.enter_context(tc.psum_pool(name="psum", bufs=8))
+        norm = stack.enter_context(tc.tile_pool(name="norm", bufs=4))
+        work = stack.enter_context(tc.tile_pool(name="work", bufs=4))
+        results = stack.enter_context(tc.tile_pool(name="results", bufs=4))
 
         x_tiles = []
         for tt in range(TOKEN_TILES):
@@ -81,15 +86,6 @@ def tile_transformerlayershard_pa_kernel(
                 )
                 w_rows[(m, g)] = w_tile
 
-        identity = resident.tile([P, P], F32, name="identity")
-        make_identity(nc, identity[:])
-        minus_half = resident.tile([P, 1], F32, name="minus_half")
-        nc.vector.memset(minus_half[:], -0.5)
-        gain = resident.tile([P, PASSES * PACK], F32, name="gain")
-        offset = resident.tile([P, PASSES * PACK], F32, name="offset")
-        nc.vector.tensor_copy(out=gain[:], in_=gain_bf[:].rearrange("p g t -> p (g t)"))
-        nc.vector.tensor_copy(out=offset[:], in_=offset_bf[:].rearrange("p g t -> p (g t)"))
-
         position = resident.tile([P, TOKEN_TILES], F32, name="position")
         nc.gpsimd.iota(
             position[:],
@@ -98,6 +94,10 @@ def tile_transformerlayershard_pa_kernel(
             channel_multiplier=1,
             allow_small_or_imprecise_dtypes=True,
         )
+        identity = resident.tile([P, P], F32, name="identity")
+        make_identity(nc, identity[:])
+        minus_half = resident.tile([P, 1], F32, name="minus_half")
+        nc.vector.memset(minus_half[:], -0.5)
         signed_freq = resident.tile([P, ANGLES], F32, name="signed_freq")
         nc.vector.memset(signed_freq[:, 0:1], -1.0)
         for doubling in range(6):
@@ -107,20 +107,16 @@ def tile_transformerlayershard_pa_kernel(
                 in0=signed_freq[:, 0:width],
                 scalar1=(-FREQ_RATIO) ** width,
             )
-        phase = resident.tile([P, 2, TOKEN_TILES, ANGLES], F32, name="phase")
-        turns = resident.tile([P, 2, TOKEN_TILES, ANGLES], F32, name="turns")
-        trig = resident.tile([P, 2, TOKEN_TILES, ANGLES], F32, name="trig")
-        phase_flat = phase[:].rearrange("p a b c -> p (a b c)")
-        turns_flat = turns[:].rearrange("p a b c -> p (a b c)")
+        phase = resident.tile([P, TOKEN_TILES, ANGLES], F32, name="phase")
+        turns = resident.tile([P, TOKEN_TILES, ANGLES], F32, name="turns")
+        cos_table = resident.tile([P, TOKEN_TILES, ANGLES], F32, name="cos_table")
+        sin_table = resident.tile([P, TOKEN_TILES, ANGLES], F32, name="sin_table")
+        phase_flat = phase[:].rearrange("p b c -> p (b c)")
+        turns_flat = turns[:].rearrange("p b c -> p (b c)")
         for tt in range(TOKEN_TILES):
             nc.vector.tensor_scalar_mul(
-                out=phase[:, 0, tt, :], in0=signed_freq[:], scalar1=position[:, tt : tt + 1]
+                out=phase[:, tt, :], in0=signed_freq[:], scalar1=position[:, tt : tt + 1]
             )
-        nc.vector.tensor_scalar_add(
-            out=phase[:, 1].rearrange("p b c -> p (b c)"),
-            in0=phase[:, 0].rearrange("p b c -> p (b c)"),
-            scalar1=-0.5 * math.pi,
-        )
         nc.vector.tensor_scalar(
             out=turns_flat,
             in0=phase_flat,
@@ -139,6 +135,17 @@ def tile_transformerlayershard_pa_kernel(
                 op0=ALU.mult,
                 op1=ALU.add,
             )
+        nc.vector.tensor_scalar(
+            out=phase_flat,
+            in0=phase_flat,
+            scalar1=PI_BELOW,
+            scalar2=-PI_BELOW,
+            op0=ALU.min,
+            op1=ALU.max,
+        )
+        nc.scalar.activation(
+            out=sin_table[:].rearrange("p b c -> p (b c)"), in_=phase_flat, func=ACT.Sin
+        )
         nc.vector.scalar_tensor_tensor(
             out=turns_flat,
             in0=phase_flat,
@@ -148,105 +155,173 @@ def tile_transformerlayershard_pa_kernel(
             op1=ALU.max,
         )
         nc.scalar.activation(
-            out=trig[:].rearrange("p a b c -> p (a b c)"),
+            out=cos_table[:].rearrange("p b c -> p (b c)"),
             in_=turns_flat,
             func=ACT.Sin,
             scale=-1.0,
             bias=0.5 * math.pi,
         )
 
-        x_codes = []
-        x_scales = []
+        w_grouped = {}
+        w_codes = {}
+        w_scales = {}
 
-        def layer_norm_tile(tt):
-            x_tile = x_tiles[tt]
+        def regroup_weight_chunk(m, c, copy):
+            for g in range(PASSES):
+                grouped = resident.tile(
+                    [P, CHUNK, PACK], BF16, name="w_grouped%d_%d_%d" % (m, c, g), align_bytes=64
+                )
+                copy(
+                    out=grouped[:].rearrange("p (a i) t -> p a t i", i=RUN),
+                    in_=w_rows[(m, g)][:, :, c * CHUNK : (c + 1) * CHUNK].rearrange(
+                        "p t (a i) -> p a t i", i=RUN
+                    ),
+                )
+                w_grouped[(m, c, g)] = grouped
+
+        def quantise_weight_chunk(m, c):
+            codes = resident.tile(
+                [P, PASSES, CHUNK], U32, name="w_codes%d_%d" % (m, c), align_bytes=64
+            )
+            scales = resident.tile(
+                [P, PASSES, CHUNK], U8, name="w_scales%d_%d" % (m, c), align_bytes=64
+            )
+            for g in range(PASSES):
+                nc.vector.quantize_mx(
+                    out=codes[:, g, :].bitcast(FP8X4),
+                    scales=scales[:, g, :],
+                    in_=w_grouped[(m, c, g)][:].rearrange("p n t -> p (n t)"),
+                )
+            w_codes[(m, c)] = codes
+            w_scales[(m, c)] = scales
+
+        rstd = []
+        shift = []
+        for tt in range(TOKEN_TILES):
             stats = small.tile([P, D // BN_STATS_MAX, BN_STATS_DIM], F32, name="stats")
             for part in range(D // BN_STATS_MAX):
                 nc.vector.bn_stats(
                     out=stats[:, part, :],
-                    in_=x_tile[:, part * BN_STATS_MAX : (part + 1) * BN_STATS_MAX],
+                    in_=x_tiles[tt][:, part * BN_STATS_MAX : (part + 1) * BN_STATS_MAX],
                 )
             mean_var = small.tile([P, 2], F32, name="mean_var")
             nc.vector.bn_aggr(out=mean_var[:], in_=stats[:].rearrange("p a b -> p (a b)"))
             var_eps = small.tile([P, 1], F32, name="var_eps")
-            nc.gpsimd.tensor_scalar_add(out=var_eps[:], in0=mean_var[:, 1:2], scalar1=EPS)
-            rstd = small.tile([P, 1], F32, name="rstd")
-            nc.gpsimd.tensor_tensor(out=rstd[:], in0=var_eps[:], in1=minus_half[:], op=ALU.pow)
-            shift = small.tile([P, 1], F32, name="shift")
-            nc.vector.scalar_tensor_tensor(
-                out=shift[:],
-                in0=mean_var[:, 0:1],
-                scalar=-1.0,
-                in1=rstd[:],
-                op0=ALU.mult,
-                op1=ALU.mult,
+            nc.vector.tensor_scalar_add(out=var_eps[:], in0=mean_var[:, 1:2], scalar1=EPS)
+            minus_mean = small.tile([P, 1], F32, name="minus_mean")
+            nc.vector.tensor_scalar_mul(out=minus_mean[:], in0=mean_var[:, 0:1], scalar1=-1.0)
+            rstd_tile = small.tile([P, 1], F32, name="rstd")
+            nc.gpsimd.tensor_tensor(
+                out=rstd_tile[:], in0=var_eps[:], in1=minus_half[:], op=ALU.pow
             )
-            z = norm.tile([P, PASSES, PACK, P], F32, name="z")
-            nc.scalar.activation(
-                out=z[:],
-                in_=x_tile[:].rearrange("q (g c t) -> q g t c", g=PASSES, t=PACK),
-                func=ACT.Identity,
-                scale=rstd[:, 0:1],
-                bias=shift[:, 0:1],
+            shift_tile = small.tile([P, 1], F32, name="shift")
+            nc.gpsimd.tensor_tensor(
+                out=shift_tile[:], in0=minus_mean[:], in1=rstd_tile[:], op=ALU.mult
             )
-            planes = norm.tile([P, PASSES, PACK, P], BF16, name="planes")
+            rstd.append(rstd_tile)
+            shift.append(shift_tile)
+
+        gain = resident.tile([P, PASSES * PACK], F32, name="gain")
+        offset = resident.tile([P, PASSES * PACK], F32, name="offset")
+        nc.vector.tensor_copy(out=gain[:], in_=gain_bf[:].rearrange("p g t -> p (g t)"))
+        nc.vector.tensor_copy(out=offset[:], in_=offset_bf[:].rearrange("p g t -> p (g t)"))
+
+        planes = resident.tile([P, PASSES, PACK, TOKENS], BF16, name="planes")
+        x_grouped = resident.tile([P, PASSES, TOKENS, PACK], BF16, name="x_grouped", align_bytes=64)
+        x_codes = resident.tile([P, PASSES, TOKENS], U32, name="x_codes", align_bytes=64)
+        x_scales = resident.tile([P, PASSES, TOKENS], U8, name="x_scales", align_bytes=64)
+
+        with tc.psum_pool(name="transposed", bufs=1) as transposed:
+            z_t = {}
             for g in range(PASSES):
-                z_t = psum.tile([P, PACK, P], F32, name="z_t", tag="bank")
                 for t in range(PACK):
-                    nc.tensor.transpose(z_t[:, t, :], z[:, g, t, :], identity[:])
-                for t in range(PACK):
-                    nc.scalar.activation(
-                        out=planes[:, g, t, :],
-                        in_=z_t[:, t, :],
-                        func=ACT.Identity,
-                        scale=gain[:, g * PACK + t : g * PACK + t + 1],
-                        bias=offset[:, g * PACK + t : g * PACK + t + 1],
-                    )
-            grouped = norm.tile([P, PASSES, P, PACK], BF16, name="x_grouped", align_bytes=64)
-            nc.vector.tensor_copy(out=grouped[:], in_=planes[:].rearrange("p g t r -> p g r t"))
-            codes = resident.tile([P, PASSES, P], U32, name="x_codes%d" % tt, align_bytes=64)
-            scales = resident.tile([P, PASSES, P], U8, name="x_scales%d" % tt, align_bytes=64)
+                    z_t[(g, t)] = transposed.tile([P, TOKENS], F32, name="z_t%d_%d" % (g, t))
+            for tt in range(TOKEN_TILES):
+                z = norm.tile([P, PASSES, PACK, P], F32, name="z")
+                nc.scalar.activation(
+                    out=z[:],
+                    in_=x_tiles[tt][:].rearrange("q (g c t) -> q g t c", g=PASSES, t=PACK),
+                    func=ACT.Identity,
+                    scale=rstd[tt][:, 0:1],
+                    bias=shift[tt][:, 0:1],
+                )
+                for g in range(PASSES):
+                    for t in range(PACK):
+                        nc.tensor.transpose(
+                            z_t[(g, t)][:, tt * P : (tt + 1) * P], z[:, g, t, :], identity[:]
+                        )
+
+            regroup_weight_chunk(0, 0, nc.vector.tensor_copy)
+            quantise_weight_chunk(0, 0)
+
+            for t in range(PACK):
+                nc.vector.tensor_scalar(
+                    out=planes[:, 0, t, :],
+                    in0=z_t[(0, t)][:],
+                    scalar1=gain[:, t : t + 1],
+                    scalar2=offset[:, t : t + 1],
+                    op0=ALU.mult,
+                    op1=ALU.add,
+                )
+                nc.scalar.activation(
+                    out=planes[:, 1, t, :],
+                    in_=z_t[(1, t)][:],
+                    func=ACT.Identity,
+                    scale=gain[:, PACK + t : PACK + t + 1],
+                    bias=offset[:, PACK + t : PACK + t + 1],
+                )
+
+        for g in range(PASSES):
+            nc.vector.tensor_copy(
+                out=x_grouped[:, g].rearrange("p (a i) t -> p a t i", i=RUN),
+                in_=planes[:, g].rearrange("p t (a i) -> p a t i", i=RUN),
+            )
+        for g in range(PASSES):
             nc.vector.quantize_mx(
-                out=codes[:].rearrange("p g r -> p (g r)").bitcast(FP8X4),
-                scales=scales[:].rearrange("p g r -> p (g r)"),
-                in_=grouped[:].rearrange("p g r t -> p (g r t)"),
+                out=x_codes[:, g, :].bitcast(FP8X4),
+                scales=x_scales[:, g, :],
+                in_=x_grouped[:, g].rearrange("p r t -> p (r t)"),
             )
-            x_codes.append(codes)
-            x_scales.append(scales)
 
-        w_codes = {}
-        w_scales = {}
+        for m, c in chunks[1:]:
+            regroup_weight_chunk(m, c, nc.scalar.copy)
 
-        def quantise_weight_chunk(m, c, copy):
-            codes = resident.tile([P, PASSES, CHUNK], U32, name="w_codes%d_%d" % (m, c), align_bytes=64)
-            scales = resident.tile([P, PASSES, CHUNK], U8, name="w_scales%d_%d" % (m, c), align_bytes=64)
+        rope_banks = stack.enter_context(
+            tc.psum_pool(name="rope_banks", bufs=LOOKAHEAD + 1, reuse_waits="tile")
+        )
+        plain_banks = stack.enter_context(
+            tc.psum_pool(name="plain_banks", bufs=LOOKAHEAD + 1, reuse_waits="tile")
+        )
+
+        jobs = [(m, c, tt) for m, c in chunks for tt in range(TOKEN_TILES)]
+        banks = {}
+
+        def multiply(m, c, tt):
+            pool = rope_banks if m < 2 else plain_banks
+            acc = pool.tile([P, CHUNK], F32, name="acc")
             for g in range(PASSES):
-                grouped = regroup.tile([P, CHUNK, PACK], BF16, name="w_grouped", align_bytes=64)
-                copy(
-                    out=grouped[:].rearrange("p (a i) t -> p a t i", i=4),
-                    in_=w_rows[(m, g)][:, :, c * CHUNK : (c + 1) * CHUNK].rearrange(
-                        "p t (a i) -> p a t i", i=4
-                    ),
+                nc.tensor.matmul_mx(
+                    out=acc[:],
+                    lhsT=x_codes[:, g, tt * P : (tt + 1) * P].bitcast(FP8X4),
+                    lhsT_scale=x_scales[:, g, tt * P : (tt + 1) * P],
+                    rhs=w_codes[(m, c)][:, g, :].bitcast(FP8X4),
+                    rhs_scale=w_scales[(m, c)][:, g, :],
+                    start=(g == 0),
+                    stop=(g == PASSES - 1),
                 )
-                nc.vector.quantize_mx(
-                    out=codes[:, g, :].bitcast(FP8X4),
-                    scales=scales[:, g, :],
-                    in_=grouped[:].rearrange("p n t -> p (n t)"),
-                )
-            w_codes[(m, c)] = codes
-            w_scales[(m, c)] = scales
+            banks[(m, c, tt)] = acc
 
         def rope(acc, tt, result):
             straight = work.tile([P, CHUNK], F32, name="straight")
             nc.vector.tensor_tensor(
                 out=straight[:].rearrange("p (r m) -> p r m", m=ANGLES),
                 in0=acc[:].rearrange("p (r m) -> p r m", m=ANGLES),
-                in1=trig[:, 0, tt, :].unsqueeze(1).to_broadcast([P, REPEATS, ANGLES]),
+                in1=cos_table[:, tt, :].unsqueeze(1).to_broadcast([P, REPEATS, ANGLES]),
                 op=ALU.mult,
             )
             crossed = work.tile([P, 2, CHUNK // 2], F32, name="crossed")
             y_pairs = acc[:].rearrange("p (r i two) -> p r i two", r=REPEATS, two=2)
-            sin_pairs = trig[:, 1, tt, :].rearrange("p (i two) -> p i two", two=2)
+            sin_pairs = sin_table[:, tt, :].rearrange("p (i two) -> p i two", two=2)
             for parity in range(2):
                 nc.vector.tensor_tensor(
                     out=crossed[:, parity, :].rearrange("p (r i) -> p r i", r=REPEATS),
@@ -263,34 +338,26 @@ def tile_transformerlayershard_pa_kernel(
                 op=ALU.add,
             )
 
-        def project_chunk(m, c):
-            for tt in range(TOKEN_TILES):
-                acc = psum.tile([P, CHUNK], F32, name="acc", tag="bank")
-                for g in range(PASSES):
-                    nc.tensor.matmul_mx(
-                        out=acc[:],
-                        lhsT=x_codes[tt][:, g, :].bitcast(FP8X4),
-                        lhsT_scale=x_scales[tt][:, g, :],
-                        rhs=w_codes[(m, c)][:, g, :].bitcast(FP8X4),
-                        rhs_scale=w_scales[(m, c)][:, g, :],
-                        start=(g == 0),
-                        stop=(g == PASSES - 1),
-                    )
-                result = results.tile([P, CHUNK], F32, name="result")
-                if m < 2:
-                    rope(acc, tt, result)
-                else:
-                    nc.scalar.copy(out=result[:], in_=acc[:])
-                nc.sync.dma_start(
-                    out=out_rows[m][tt * P : (tt + 1) * P, c * CHUNK : (c + 1) * CHUNK],
-                    in_=result[:],
-                )
+        def finish(m, c, tt):
+            acc = banks[(m, c, tt)]
+            rows = out_rows[m][tt * P : (tt + 1) * P, c * CHUNK : (c + 1) * CHUNK]
+            if m < 2:
+                turned = results.tile([P, CHUNK], F32, name="turned")
+                rope(acc, tt, turned)
+                nc.sync.dma_start(out=rows, in_=turned[:])
+            else:
+                plain = results.tile([P, CHUNK], F32, name="plain")
+                nc.scalar.copy(out=plain[:], in_=acc[:])
+                nc.scalar.dma_start(out=rows, in_=plain[:])
 
-        for tt in range(TOKEN_TILES):
-            layer_norm_tile(tt)
-        chunks = [(m, c) for m in range(3) for c in range(CHUNKS)]
-        quantise_weight_chunk(0, 0, nc.vector.tensor_copy)
-        for index in range(len(chunks)):
-            if index + 1 < len(chunks):
-                quantise_weight_chunk(chunks[index + 1][0], chunks[index + 1][1], nc.scalar.copy)
-            project_chunk(chunks[index][0], chunks[index][1])
+        quantised = 1
+        for job in jobs[:LOOKAHEAD]:
+            multiply(job[0], job[1], job[2])
+        for index in range(len(jobs)):
+            if index + LOOKAHEAD < len(jobs):
+                ahead = jobs[index + LOOKAHEAD]
+                multiply(ahead[0], ahead[1], ahead[2])
+            finish(jobs[index][0], jobs[index][1], jobs[index][2])
+            if index % QUANTISE_EVERY == 0 and quantised < len(chunks):
+                quantise_weight_chunk(chunks[quantised][0], chunks[quantised][1])
+                quantised += 1

@@ -319,24 +319,17 @@ def tile_transformerlayershard_pa_kernel(
                 in1=cos_table[:, tt, :].unsqueeze(1).to_broadcast([P, REPEATS, ANGLES]),
                 op=ALU.mult,
             )
-            crossed = work.tile([P, 2, CHUNK // 2], F32, name="crossed")
-            y_pairs = acc[:].rearrange("p (r i two) -> p r i two", r=REPEATS, two=2)
-            sin_pairs = sin_table[:, tt, :].rearrange("p (i two) -> p i two", two=2)
-            for parity in range(2):
-                nc.vector.tensor_tensor(
-                    out=crossed[:, parity, :].rearrange("p (r i) -> p r i", r=REPEATS),
-                    in0=y_pairs[:, :, :, 1 - parity],
-                    in1=sin_pairs[:, :, parity]
-                    .unsqueeze(1)
-                    .to_broadcast([P, REPEATS, ANGLES // 2]),
-                    op=ALU.mult,
-                )
-            nc.gpsimd.tensor_tensor(
-                out=result[:].rearrange("p (n two) -> p n two", two=2),
-                in0=straight[:].rearrange("p (n two) -> p n two", two=2),
-                in1=crossed[:].rearrange("p two n -> p n two"),
-                op=ALU.add,
+            crossed = work.tile([P, CHUNK], F32, name="crossed")
+            nc.vector.tensor_tensor(
+                out=crossed[:].rearrange("p (r i two) -> p r i two", r=REPEATS, two=2),
+                in0=acc[:].rearrange("p (r i two) -> p r i two", r=REPEATS, two=2)[:, :, :, ::-1],
+                in1=sin_table[:, tt, :]
+                .rearrange("p (i two) -> p i two", two=2)
+                .unsqueeze(1)
+                .to_broadcast([P, REPEATS, ANGLES // 2, 2]),
+                op=ALU.mult,
             )
+            nc.gpsimd.tensor_tensor(out=result[:], in0=straight[:], in1=crossed[:], op=ALU.add)
 
         def finish(m, c, tt):
             acc = banks[(m, c, tt)]

@@ -36,7 +36,8 @@ TWO_PI_LOW = 2.0 * math.pi - TWO_PI_HIGH
 PI_BELOW = 3.1415925
 
 LOOKAHEAD = 3
-QUANTISE_EVERY = 3
+QUANTISE_EVERY = 2
+VECTOR_PIECES = 3
 
 FLOPS = 2 * TOKENS * D * 3 * E
 
@@ -48,7 +49,8 @@ def tile_transformerlayershard_pa_kernel(
     weights = (Wq, Wk, Wv)
     out_rows = [o.rearrange("s h d -> s (h d)") for o in (out_0, out_1, out_2)]
     x_rows = x.rearrange("b s d -> (b s) d")
-    chunks = [(m, c) for m in range(3) for c in range(CHUNKS)]
+    chunks = [(0, c) for c in range(CHUNKS)] + [(m, c) for c in range(CHUNKS) for m in (1, 2)]
+    pieces = [(m, c, g) for m, c in chunks for g in range(PASSES)]
 
     with ExitStack() as stack:
         stack.enter_context(tc.manual_schedule())
@@ -98,6 +100,8 @@ def tile_transformerlayershard_pa_kernel(
         make_identity(nc, identity[:])
         minus_half = resident.tile([P, 1], F32, name="minus_half")
         nc.vector.memset(minus_half[:], -0.5)
+        table_warmer = resident.tile([P, 1], F32, name="table_warmer")
+        nc.scalar.activation(out=table_warmer[:], in_=minus_half[:], func=ACT.Sin)
         signed_freq = resident.tile([P, ANGLES], F32, name="signed_freq")
         nc.vector.memset(signed_freq[:, 0:1], -1.0)
         for doubling in range(6):
@@ -117,16 +121,23 @@ def tile_transformerlayershard_pa_kernel(
             nc.vector.tensor_scalar_mul(
                 out=phase[:, tt, :], in0=signed_freq[:], scalar1=position[:, tt : tt + 1]
             )
-        nc.vector.tensor_scalar(
-            out=turns_flat,
-            in0=phase_flat,
-            scalar1=0.5 / math.pi,
-            scalar2=ROUND_MAGIC,
-            op0=ALU.mult,
-            op1=ALU.add,
-        )
-        nc.vector.tensor_scalar_sub(out=turns_flat, in0=turns_flat, scalar1=ROUND_MAGIC)
-        for part_of_two_pi in (TWO_PI_HIGH, TWO_PI_LOW):
+        gain = resident.tile([P, PASSES * PACK], F32, name="gain")
+        offset = resident.tile([P, PASSES * PACK], F32, name="offset")
+
+        def count_turns():
+            nc.vector.tensor_scalar(
+                out=turns_flat,
+                in0=phase_flat,
+                scalar1=0.5 / math.pi,
+                scalar2=ROUND_MAGIC,
+                op0=ALU.mult,
+                op1=ALU.add,
+            )
+
+        def round_turns():
+            nc.vector.tensor_scalar_sub(out=turns_flat, in0=turns_flat, scalar1=ROUND_MAGIC)
+
+        def take_off_turns(part_of_two_pi):
             nc.vector.scalar_tensor_tensor(
                 out=phase_flat,
                 in0=turns_flat,
@@ -135,96 +146,109 @@ def tile_transformerlayershard_pa_kernel(
                 op0=ALU.mult,
                 op1=ALU.add,
             )
-        nc.vector.tensor_scalar(
-            out=phase_flat,
-            in0=phase_flat,
-            scalar1=PI_BELOW,
-            scalar2=-PI_BELOW,
-            op0=ALU.min,
-            op1=ALU.max,
-        )
-        nc.scalar.activation(
-            out=sin_table[:].rearrange("p b c -> p (b c)"), in_=phase_flat, func=ACT.Sin
-        )
-        nc.vector.scalar_tensor_tensor(
-            out=turns_flat,
-            in0=phase_flat,
-            scalar=-1.0,
-            in1=phase_flat,
-            op0=ALU.mult,
-            op1=ALU.max,
-        )
-        nc.scalar.activation(
-            out=cos_table[:].rearrange("p b c -> p (b c)"),
-            in_=turns_flat,
-            func=ACT.Sin,
-            scale=-1.0,
-            bias=0.5 * math.pi,
-        )
+
+        def clamp_phase():
+            nc.vector.tensor_scalar(
+                out=phase_flat,
+                in0=phase_flat,
+                scalar1=PI_BELOW,
+                scalar2=-PI_BELOW,
+                op0=ALU.min,
+                op1=ALU.max,
+            )
+
+        def absolute_phase():
+            nc.vector.scalar_tensor_tensor(
+                out=turns_flat,
+                in0=phase_flat,
+                scalar=-1.0,
+                in1=phase_flat,
+                op0=ALU.mult,
+                op1=ALU.max,
+            )
+
+        small_steps = [
+            count_turns,
+            round_turns,
+            lambda: take_off_turns(TWO_PI_HIGH),
+            lambda: take_off_turns(TWO_PI_LOW),
+            clamp_phase,
+            absolute_phase,
+            lambda: nc.vector.tensor_copy(out=gain[:], in_=gain_bf[:].rearrange("p g t -> p (g t)")),
+            lambda: nc.vector.tensor_copy(
+                out=offset[:], in_=offset_bf[:].rearrange("p g t -> p (g t)")
+            ),
+        ]
 
         w_grouped = {}
         w_codes = {}
         w_scales = {}
 
-        def regroup_weight_chunk(m, c, copy):
-            for g in range(PASSES):
-                grouped = resident.tile(
-                    [P, CHUNK, PACK], BF16, name="w_grouped%d_%d_%d" % (m, c, g), align_bytes=64
-                )
-                copy(
-                    out=grouped[:].rearrange("p (a i) t -> p a t i", i=RUN),
-                    in_=w_rows[(m, g)][:, :, c * CHUNK : (c + 1) * CHUNK].rearrange(
-                        "p t (a i) -> p a t i", i=RUN
-                    ),
-                )
-                w_grouped[(m, c, g)] = grouped
-
-        def quantise_weight_chunk(m, c):
-            codes = resident.tile(
-                [P, PASSES, CHUNK], U32, name="w_codes%d_%d" % (m, c), align_bytes=64
+        def regroup_weight_piece(index):
+            m, c, g = pieces[index]
+            copy = nc.vector.tensor_copy if index < VECTOR_PIECES else nc.scalar.copy
+            grouped = resident.tile(
+                [P, CHUNK, PACK], BF16, name="w_grouped%d_%d_%d" % (m, c, g), align_bytes=64
             )
-            scales = resident.tile(
-                [P, PASSES, CHUNK], U8, name="w_scales%d_%d" % (m, c), align_bytes=64
+            copy(
+                out=grouped[:].rearrange("p (a i) t -> p a t i", i=RUN),
+                in_=w_rows[(m, g)][:, :, c * CHUNK : (c + 1) * CHUNK].rearrange(
+                    "p t (a i) -> p a t i", i=RUN
+                ),
             )
-            for g in range(PASSES):
-                nc.vector.quantize_mx(
-                    out=codes[:, g, :].bitcast(FP8X4),
-                    scales=scales[:, g, :],
-                    in_=w_grouped[(m, c, g)][:].rearrange("p n t -> p (n t)"),
-                )
-            w_codes[(m, c)] = codes
-            w_scales[(m, c)] = scales
+            w_grouped[(m, c, g)] = grouped
 
+        def quantise_weight_piece(index):
+            m, c, g = pieces[index]
+            if g == 0:
+                w_codes[(m, c)] = resident.tile(
+                    [P, PASSES, CHUNK], U32, name="w_codes%d_%d" % (m, c), align_bytes=64
+                )
+                w_scales[(m, c)] = resident.tile(
+                    [P, PASSES, CHUNK], U8, name="w_scales%d_%d" % (m, c), align_bytes=64
+                )
+            nc.vector.quantize_mx(
+                out=w_codes[(m, c)][:, g, :].bitcast(FP8X4),
+                scales=w_scales[(m, c)][:, g, :],
+                in_=w_grouped[(m, c, g)][:].rearrange("p n t -> p (n t)"),
+            )
+
+        stats = []
+        mean_var = []
         rstd = []
         shift = []
-        for tt in range(TOKEN_TILES):
-            stats = small.tile([P, D // BN_STATS_MAX, BN_STATS_DIM], F32, name="stats")
-            for part in range(D // BN_STATS_MAX):
-                nc.vector.bn_stats(
-                    out=stats[:, part, :],
-                    in_=x_tiles[tt][:, part * BN_STATS_MAX : (part + 1) * BN_STATS_MAX],
-                )
-            mean_var = small.tile([P, 2], F32, name="mean_var")
-            nc.vector.bn_aggr(out=mean_var[:], in_=stats[:].rearrange("p a b -> p (a b)"))
-            var_eps = small.tile([P, 1], F32, name="var_eps")
-            nc.vector.tensor_scalar_add(out=var_eps[:], in0=mean_var[:, 1:2], scalar1=EPS)
-            minus_mean = small.tile([P, 1], F32, name="minus_mean")
-            nc.vector.tensor_scalar_mul(out=minus_mean[:], in0=mean_var[:, 0:1], scalar1=-1.0)
-            rstd_tile = small.tile([P, 1], F32, name="rstd")
-            nc.gpsimd.tensor_tensor(
-                out=rstd_tile[:], in0=var_eps[:], in1=minus_half[:], op=ALU.pow
-            )
-            shift_tile = small.tile([P, 1], F32, name="shift")
-            nc.gpsimd.tensor_tensor(
-                out=shift_tile[:], in0=minus_mean[:], in1=rstd_tile[:], op=ALU.mult
-            )
-            rstd.append(rstd_tile)
-            shift.append(shift_tile)
 
-        gain = resident.tile([P, PASSES * PACK], F32, name="gain")
-        offset = resident.tile([P, PASSES * PACK], F32, name="offset")
-        nc.vector.tensor_copy(out=gain[:], in_=gain_bf[:].rearrange("p g t -> p (g t)"))
-        nc.vector.tensor_copy(out=offset[:], in_=offset_bf[:].rearrange("p g t -> p (g t)"))
+        def measure(tt, part):
+            if part == 0:
+                stats.append(small.tile([P, D // BN_STATS_MAX, BN_STATS_DIM], F32, name="stats"))
+            nc.vector.bn_stats(
+                out=stats[tt][:, part, :],
+                in_=x_tiles[tt][:, part * BN_STATS_MAX : (part + 1) * BN_STATS_MAX],
+            )
+
+        def aggregate(tt):
+            mean_var.append(small.tile([P, 2], F32, name="mean_var"))
+            nc.vector.bn_aggr(out=mean_var[tt][:], in_=stats[tt][:].rearrange("p a b -> p (a b)"))
+
+        def scale_and_shift(tt):
+            var_eps = small.tile([P, 1], F32, name="var_eps")
+            nc.vector.tensor_scalar_add(out=var_eps[:], in0=mean_var[tt][:, 1:2], scalar1=EPS)
+            minus_mean = small.tile([P, 1], F32, name="minus_mean")
+            nc.vector.tensor_scalar_mul(out=minus_mean[:], in0=mean_var[tt][:, 0:1], scalar1=-1.0)
+            rstd.append(small.tile([P, 1], F32, name="rstd"))
+            nc.gpsimd.tensor_tensor(out=rstd[tt][:], in0=var_eps[:], in1=minus_half[:], op=ALU.pow)
+            shift.append(small.tile([P, 1], F32, name="shift"))
+            nc.gpsimd.tensor_tensor(out=shift[tt][:], in0=minus_mean[:], in1=rstd[tt][:], op=ALU.mult)
+
+        for tt in range(TOKEN_TILES):
+            measure(tt, 0)
+            if tt > 0:
+                scale_and_shift(tt - 1)
+            small_steps[2 * tt]()
+            measure(tt, 1)
+            small_steps[2 * tt + 1]()
+            aggregate(tt)
+        scale_and_shift(TOKEN_TILES - 1)
 
         planes = resident.tile([P, PASSES, PACK, TOKENS], BF16, name="planes")
         x_grouped = resident.tile([P, PASSES, TOKENS, PACK], BF16, name="x_grouped", align_bytes=64)
@@ -238,21 +262,33 @@ def tile_transformerlayershard_pa_kernel(
                     z_t[(g, t)] = transposed.tile([P, TOKENS], F32, name="z_t%d_%d" % (g, t))
             for tt in range(TOKEN_TILES):
                 z = norm.tile([P, PASSES, PACK, P], F32, name="z")
-                nc.scalar.activation(
-                    out=z[:],
-                    in_=x_tiles[tt][:].rearrange("q (g c t) -> q g t c", g=PASSES, t=PACK),
-                    func=ACT.Identity,
-                    scale=rstd[tt][:, 0:1],
-                    bias=shift[tt][:, 0:1],
-                )
+                x_sorted = x_tiles[tt][:].rearrange("q (g c t) -> q g t c", g=PASSES, t=PACK)
                 for g in range(PASSES):
+                    nc.scalar.activation(
+                        out=z[:, g],
+                        in_=x_sorted[:, g],
+                        func=ACT.Identity,
+                        scale=rstd[tt][:, 0:1],
+                        bias=shift[tt][:, 0:1],
+                    )
                     for t in range(PACK):
                         nc.tensor.transpose(
                             z_t[(g, t)][:, tt * P : (tt + 1) * P], z[:, g, t, :], identity[:]
                         )
+            nc.scalar.activation(
+                out=sin_table[:].rearrange("p b c -> p (b c)"), in_=phase_flat, func=ACT.Sin
+            )
+            nc.scalar.activation(
+                out=cos_table[:].rearrange("p b c -> p (b c)"),
+                in_=turns_flat,
+                func=ACT.Sin,
+                scale=-1.0,
+                bias=0.5 * math.pi,
+            )
 
-            regroup_weight_chunk(0, 0, nc.vector.tensor_copy)
-            quantise_weight_chunk(0, 0)
+            regroup_weight_piece(0)
+            regroup_weight_piece(1)
+            quantise_weight_piece(0)
 
             for t in range(PACK):
                 nc.vector.tensor_scalar(
@@ -270,6 +306,7 @@ def tile_transformerlayershard_pa_kernel(
                     scale=gain[:, PACK + t : PACK + t + 1],
                     bias=offset[:, PACK + t : PACK + t + 1],
                 )
+        quantise_weight_piece(1)
 
         for g in range(PASSES):
             nc.vector.tensor_copy(
@@ -283,8 +320,8 @@ def tile_transformerlayershard_pa_kernel(
                 in_=x_grouped[:, g].rearrange("p r t -> p (r t)"),
             )
 
-        for m, c in chunks[1:]:
-            regroup_weight_chunk(m, c, nc.scalar.copy)
+        for index in range(2, len(pieces)):
+            regroup_weight_piece(index)
 
         rope_banks = stack.enter_context(
             tc.psum_pool(name="rope_banks", bufs=LOOKAHEAD + 1, reuse_waits="tile")
@@ -293,7 +330,10 @@ def tile_transformerlayershard_pa_kernel(
             tc.psum_pool(name="plain_banks", bufs=LOOKAHEAD + 1, reuse_waits="tile")
         )
 
-        jobs = [(m, c, tt) for m, c in chunks for tt in range(TOKEN_TILES)]
+        jobs = [(0, c, tt) for c in range(CHUNKS) for tt in range(TOKEN_TILES)] + [
+            (m, c, tt) for c in range(CHUNKS) for tt in range(TOKEN_TILES) for m in (1, 2)
+        ]
+        last_rope_job = max(index for index in range(len(jobs)) if jobs[index][0] < 2)
         banks = {}
 
         def multiply(m, c, tt):
@@ -311,7 +351,7 @@ def tile_transformerlayershard_pa_kernel(
                 )
             banks[(m, c, tt)] = acc
 
-        def rope(acc, tt, result):
+        def rope(acc, tt, turned, adder):
             straight = work.tile([P, CHUNK], F32, name="straight")
             nc.vector.tensor_tensor(
                 out=straight[:].rearrange("p (r m) -> p r m", m=ANGLES),
@@ -329,28 +369,33 @@ def tile_transformerlayershard_pa_kernel(
                 .to_broadcast([P, REPEATS, ANGLES // 2, 2]),
                 op=ALU.mult,
             )
-            nc.gpsimd.tensor_tensor(out=result[:], in0=straight[:], in1=crossed[:], op=ALU.add)
+            adder.tensor_tensor(out=turned[:], in0=straight[:], in1=crossed[:], op=ALU.add)
 
-        def finish(m, c, tt):
+        def finish(index):
+            m, c, tt = jobs[index]
             acc = banks[(m, c, tt)]
             rows = out_rows[m][tt * P : (tt + 1) * P, c * CHUNK : (c + 1) * CHUNK]
             if m < 2:
                 turned = results.tile([P, CHUNK], F32, name="turned")
-                rope(acc, tt, turned)
+                rope(acc, tt, turned, nc.vector if index == last_rope_job else nc.gpsimd)
                 nc.sync.dma_start(out=rows, in_=turned[:])
             else:
                 plain = results.tile([P, CHUNK], F32, name="plain")
                 nc.scalar.copy(out=plain[:], in_=acc[:])
                 nc.scalar.dma_start(out=rows, in_=plain[:])
 
-        quantised = 1
-        for job in jobs[:LOOKAHEAD]:
-            multiply(job[0], job[1], job[2])
+        quantised = 2
+        turned_banks = 0
+        for m, c, tt in jobs[:LOOKAHEAD]:
+            multiply(m, c, tt)
         for index in range(len(jobs)):
             if index + LOOKAHEAD < len(jobs):
-                ahead = jobs[index + LOOKAHEAD]
-                multiply(ahead[0], ahead[1], ahead[2])
-            finish(jobs[index][0], jobs[index][1], jobs[index][2])
-            if index % QUANTISE_EVERY == 0 and quantised < len(chunks):
-                quantise_weight_chunk(chunks[quantised][0], chunks[quantised][1])
-                quantised += 1
+                m, c, tt = jobs[index + LOOKAHEAD]
+                multiply(m, c, tt)
+            finish(index)
+            if jobs[index][0] < 2:
+                if turned_banks % QUANTISE_EVERY == 0 and quantised < len(pieces):
+                    quantise_weight_piece(quantised)
+                    quantise_weight_piece(quantised + 1)
+                    quantised += 2
+                turned_banks += 1

@@ -69,10 +69,10 @@ def tile_transformerlayershard_pa_kernel(
         gain_bf = resident.tile([P, PASSES, PACK], BF16, name="gain_bf")
         offset_bf = resident.tile([P, PASSES, PACK], BF16, name="offset_bf")
         with nc.allow_non_contiguous_dma(reason="two vectors of 1024, four values to a piece"):
-            nc.scalar.dma_start(
+            nc.sync.dma_start(
                 out=gain_bf[:], in_=ln_scale.rearrange("(g p t) -> p g t", g=PASSES, t=PACK)
             )
-            nc.scalar.dma_start(
+            nc.sync.dma_start(
                 out=offset_bf[:], in_=ln_offset.rearrange("(g p t) -> p g t", g=PASSES, t=PACK)
             )
 

@@ -37,7 +37,9 @@ PI_BELOW = 3.1415925
 
 LOOKAHEAD = 3
 QUANTISE_EVERY = 2
-VECTOR_PIECES = 3
+VECTOR_PIECES = 2
+TENSOR_PIECES = range(2, 6)
+HALF = CHUNK // 2
 
 FLOPS = 2 * TOKENS * D * 3 * E
 
@@ -98,6 +100,8 @@ def tile_transformerlayershard_pa_kernel(
         )
         identity = resident.tile([P, P], F32, name="identity")
         make_identity(nc, identity[:])
+        identity_bf = resident.tile([P, P], BF16, name="identity_bf")
+        nc.gpsimd.tensor_copy(out=identity_bf[:], in_=identity[:])
         minus_half = resident.tile([P, 1], F32, name="minus_half")
         nc.vector.memset(minus_half[:], -0.5)
         table_warmer = resident.tile([P, 1], F32, name="table_warmer")
@@ -308,6 +312,54 @@ def tile_transformerlayershard_pa_kernel(
                 )
         quantise_weight_piece(1)
 
+        rope_banks = stack.enter_context(
+            tc.psum_pool(name="rope_banks", bufs=LOOKAHEAD + 1, reuse_waits="tile")
+        )
+        plain_banks = stack.enter_context(
+            tc.psum_pool(name="plain_banks", bufs=LOOKAHEAD + 1, reuse_waits="tile")
+        )
+
+        halves = [(index, half) for index in TENSOR_PIECES for half in range(2)]
+        half_banks = {}
+
+        def regroup_half(number):
+            index, half = halves[number]
+            m, c, g = pieces[index]
+            bank = plain_banks.tile([P, HALF * PACK], BF16, name="acc")
+            for part in range(2):
+                first = c * CHUNK + half * HALF + part * P
+                nc.tensor.matmul(
+                    out=bank[:, part * P * PACK : (part + 1) * P * PACK].rearrange(
+                        "p (n t) -> p n t", t=PACK
+                    ),
+                    lhsT=identity_bf[:],
+                    rhs=w_rows[(m, g)][:, :, first : first + P].rearrange("p t n -> p n t"),
+                    start=True,
+                    stop=True,
+                )
+            half_banks[number] = bank
+
+        def copy_half(number):
+            index, half = halves[number]
+            if half == 0:
+                w_grouped[pieces[index]] = resident.tile(
+                    [P, CHUNK, PACK], BF16, name="w_grouped%d_%d_%d" % pieces[index], align_bytes=64
+                )
+            nc.scalar.copy(
+                out=w_grouped[pieces[index]][:, half * HALF : (half + 1) * HALF, :].rearrange(
+                    "p n t -> p (n t)"
+                ),
+                in_=half_banks[number][:],
+            )
+
+        for number in range(4):
+            regroup_half(number)
+        for number in range(2):
+            copy_half(number)
+            regroup_half(number + 4)
+        for number in range(2, 6):
+            copy_half(number)
+
         for g in range(PASSES):
             nc.vector.tensor_copy(
                 out=x_grouped[:, g].rearrange("p (a i) t -> p a t i", i=RUN),
@@ -320,15 +372,7 @@ def tile_transformerlayershard_pa_kernel(
                 in_=x_grouped[:, g].rearrange("p r t -> p (r t)"),
             )
 
-        for index in range(2, len(pieces)):
-            regroup_weight_piece(index)
-
-        rope_banks = stack.enter_context(
-            tc.psum_pool(name="rope_banks", bufs=LOOKAHEAD + 1, reuse_waits="tile")
-        )
-        plain_banks = stack.enter_context(
-            tc.psum_pool(name="plain_banks", bufs=LOOKAHEAD + 1, reuse_waits="tile")
-        )
+        quantise_weight_piece(2)
 
         jobs = [(0, c, tt) for c in range(CHUNKS) for tt in range(TOKEN_TILES)] + [
             (m, c, tt) for c in range(CHUNKS) for tt in range(TOKEN_TILES) for m in (1, 2)
@@ -384,10 +428,16 @@ def tile_transformerlayershard_pa_kernel(
                 nc.scalar.copy(out=plain[:], in_=acc[:])
                 nc.scalar.dma_start(out=rows, in_=plain[:])
 
-        quantised = 2
+        quantised = 3
         turned_banks = 0
         for m, c, tt in jobs[:LOOKAHEAD]:
             multiply(m, c, tt)
+        for number in range(6, 8):
+            regroup_half(number)
+        for number in range(6, 8):
+            copy_half(number)
+        for index in range(TENSOR_PIECES.stop, len(pieces)):
+            regroup_weight_piece(index)
         for index in range(len(jobs)):
             if index + LOOKAHEAD < len(jobs):
                 m, c, tt = jobs[index + LOOKAHEAD]
@@ -395,7 +445,7 @@ def tile_transformerlayershard_pa_kernel(
             finish(index)
             if jobs[index][0] < 2:
                 if turned_banks % QUANTISE_EVERY == 0 and quantised < len(pieces):
-                    quantise_weight_piece(quantised)
-                    quantise_weight_piece(quantised + 1)
-                    quantised += 2
+                    for index in range(quantised, quantised + 2 - quantised % 2):
+                        quantise_weight_piece(index)
+                    quantised += 2 - quantised % 2
                 turned_banks += 1

@@ -24,6 +24,7 @@ CHUNK = 512
 CHUNKS = E // CHUNK
 ANGLES = 64
 REPEATS = CHUNK // ANGLES
+LINE = 8
 RUN = 4
 EPS = 1e-5
 BN_STATS_MAX = 512
@@ -330,10 +331,12 @@ def tile_transformerlayershard_pa_kernel(
                 first = c * CHUNK + half * HALF + part * P
                 nc.tensor.matmul(
                     out=bank[:, part * P * PACK : (part + 1) * P * PACK].rearrange(
-                        "p (n t) -> p n t", t=PACK
+                        "p (a i t) -> p a t i", i=LINE, t=PACK
                     ),
                     lhsT=identity_bf[:],
-                    rhs=w_rows[(m, g)][:, :, first : first + P].rearrange("p t n -> p n t"),
+                    rhs=w_rows[(m, g)][:, :, first : first + P].rearrange(
+                        "p t (a i) -> p a t i", i=LINE
+                    ),
                     start=True,
                     stop=True,
                 )

@@ -24,7 +24,6 @@ CHUNK = 512
 CHUNKS = E // CHUNK
 ANGLES = 64
 REPEATS = CHUNK // ANGLES
-LINE = 8
 RUN = 4
 EPS = 1e-5
 BN_STATS_MAX = 512
@@ -38,8 +37,8 @@ PI_BELOW = 3.1415925
 
 LOOKAHEAD = 3
 QUANTISE_EVERY = 2
-VECTOR_PIECES = 2
-TENSOR_PIECES = range(2, 6)
+VECTOR_PIECES = 3
+TENSOR_PIECES = (4, 6, 8, 10)
 HALF = CHUNK // 2
 
 FLOPS = 2 * TOKENS * D * 3 * E
@@ -331,12 +330,10 @@ def tile_transformerlayershard_pa_kernel(
                 first = c * CHUNK + half * HALF + part * P
                 nc.tensor.matmul(
                     out=bank[:, part * P * PACK : (part + 1) * P * PACK].rearrange(
-                        "p (a i t) -> p a t i", i=LINE, t=PACK
+                        "p (n t) -> p t n", t=PACK
                     ),
                     lhsT=identity_bf[:],
-                    rhs=w_rows[(m, g)][:, :, first : first + P].rearrange(
-                        "p t (a i) -> p a t i", i=LINE
-                    ),
+                    rhs=w_rows[(m, g)][:, :, first : first + P],
                     start=True,
                     stop=True,
                 )
@@ -355,13 +352,16 @@ def tile_transformerlayershard_pa_kernel(
                 in_=half_banks[number][:],
             )
 
-        for number in range(4):
-            regroup_half(number)
-        for number in range(2):
-            copy_half(number)
-            regroup_half(number + 4)
-        for number in range(2, 6):
-            copy_half(number)
+        def copy_piece(index):
+            first = 2 * TENSOR_PIECES.index(index)
+            copy_half(first)
+            copy_half(first + 1)
+            regroup_weight_piece(index + 1)
+
+        regroup_half(0)
+        regroup_half(1)
+        regroup_weight_piece(3)
+        copy_piece(4)
 
         for g in range(PASSES):
             nc.vector.tensor_copy(
@@ -375,7 +375,7 @@ def tile_transformerlayershard_pa_kernel(
                 in_=x_grouped[:, g].rearrange("p r t -> p (r t)"),
             )
 
-        quantise_weight_piece(2)
+        regroup_weight_piece(2)
 
         jobs = [(0, c, tt) for c in range(CHUNKS) for tt in range(TOKEN_TILES)] + [
             (m, c, tt) for c in range(CHUNKS) for tt in range(TOKEN_TILES) for m in (1, 2)
@@ -431,24 +431,26 @@ def tile_transformerlayershard_pa_kernel(
                 nc.scalar.copy(out=plain[:], in_=acc[:])
                 nc.scalar.dma_start(out=rows, in_=plain[:])
 
-        quantised = 3
+        quantised = 2
         turned_banks = 0
         for m, c, tt in jobs[:LOOKAHEAD]:
             multiply(m, c, tt)
-        for number in range(6, 8):
-            regroup_half(number)
-        for number in range(6, 8):
-            copy_half(number)
-        for index in range(TENSOR_PIECES.stop, len(pieces)):
-            regroup_weight_piece(index)
+        regroup_half(2)
+        regroup_half(3)
+        copy_piece(6)
+        halves_after = {0: 4, 1: 5, 3: 6, 4: 7}
         for index in range(len(jobs)):
             if index + LOOKAHEAD < len(jobs):
                 m, c, tt = jobs[index + LOOKAHEAD]
                 multiply(m, c, tt)
+            if index in halves_after:
+                regroup_half(halves_after[index])
+                if halves_after[index] % 2 == 1:
+                    copy_piece(halves[halves_after[index]][0])
             finish(index)
             if jobs[index][0] < 2:
                 if turned_banks % QUANTISE_EVERY == 0 and quantised < len(pieces):
-                    for index in range(quantised, quantised + 2 - quantised % 2):
-                        quantise_weight_piece(index)
-                    quantised += 2 - quantised % 2
+                    quantise_weight_piece(quantised)
+                    quantise_weight_piece(quantised + 1)
+                    quantised += 2
                 turned_banks += 1

@@ -37,7 +37,7 @@ PI_BELOW = 3.1415925
 
 LOOKAHEAD = 3
 QUANTISE_EVERY = 2
-VECTOR_PIECES = 3
+VECTOR_PIECES = 2
 TENSOR_PIECES = (4, 6, 8, 10)
 HALF = CHUNK // 2
 
@@ -360,6 +360,7 @@ def tile_transformerlayershard_pa_kernel(
 
         regroup_half(0)
         regroup_half(1)
+        regroup_weight_piece(2)
         regroup_weight_piece(3)
         copy_piece(4)
 
@@ -375,7 +376,7 @@ def tile_transformerlayershard_pa_kernel(
                 in_=x_grouped[:, g].rearrange("p r t -> p (r t)"),
             )
 
-        regroup_weight_piece(2)
+        quantise_weight_piece(2)
 
         jobs = [(0, c, tt) for c in range(CHUNKS) for tt in range(TOKEN_TILES)] + [
             (m, c, tt) for c in range(CHUNKS) for tt in range(TOKEN_TILES) for m in (1, 2)
@@ -431,7 +432,7 @@ def tile_transformerlayershard_pa_kernel(
                 nc.scalar.copy(out=plain[:], in_=acc[:])
                 nc.scalar.dma_start(out=rows, in_=plain[:])
 
-        quantised = 2
+        quantised = 3
         turned_banks = 0
         for m, c, tt in jobs[:LOOKAHEAD]:
             multiply(m, c, tt)
@@ -450,7 +451,7 @@ def tile_transformerlayershard_pa_kernel(
             finish(index)
             if jobs[index][0] < 2:
                 if turned_banks % QUANTISE_EVERY == 0 and quantised < len(pieces):
-                    quantise_weight_piece(quantised)
-                    quantise_weight_piece(quantised + 1)
-                    quantised += 2
+                    for piece in range(quantised, quantised + 2 - quantised % 2):
+                        quantise_weight_piece(piece)
+                    quantised += 2 - quantised % 2
                 turned_banks += 1

@@ -36,7 +36,6 @@ TWO_PI_LOW = 2.0 * math.pi - TWO_PI_HIGH
 PI_BELOW = 3.1415925
 
 LOOKAHEAD = 3
-QUANTISE_EVERY = 2
 VECTOR_PIECES = 2
 TENSOR_PIECES = (4, 6, 8, 10)
 HALF = CHUNK // 2
@@ -59,8 +58,9 @@ def tile_transformerlayershard_pa_kernel(
         resident = stack.enter_context(tc.tile_pool(name="resident", bufs=1))
         small = stack.enter_context(tc.tile_pool(name="small", bufs=4))
         norm = stack.enter_context(tc.tile_pool(name="norm", bufs=4))
-        work = stack.enter_context(tc.tile_pool(name="work", bufs=4))
-        results = stack.enter_context(tc.tile_pool(name="results", bufs=4))
+        work = stack.enter_context(tc.tile_pool(name="work", bufs=3))
+        results = stack.enter_context(tc.tile_pool(name="results", bufs=3))
+        plain_results = stack.enter_context(tc.tile_pool(name="plain_results", bufs=4))
 
         x_tiles = []
         for tt in range(TOKEN_TILES):
@@ -399,17 +399,20 @@ def tile_transformerlayershard_pa_kernel(
                 )
             banks[(m, c, tt)] = acc
 
-        def rope(acc, tt, turned, adder):
-            straight = work.tile([P, CHUNK], F32, name="straight")
+        pair = {}
+
+        def rope(acc, tt, part):
+            if part == 0:
+                pair["straight"] = work.tile([P, 2, CHUNK], F32, name="straight")
+                pair["crossed"] = work.tile([P, 2, CHUNK], F32, name="crossed")
             nc.vector.tensor_tensor(
-                out=straight[:].rearrange("p (r m) -> p r m", m=ANGLES),
+                out=pair["straight"][:, part].rearrange("p (r m) -> p r m", m=ANGLES),
                 in0=acc[:].rearrange("p (r m) -> p r m", m=ANGLES),
                 in1=cos_table[:, tt, :].unsqueeze(1).to_broadcast([P, REPEATS, ANGLES]),
                 op=ALU.mult,
             )
-            crossed = work.tile([P, CHUNK], F32, name="crossed")
             nc.vector.tensor_tensor(
-                out=crossed[:].rearrange("p (r i two) -> p r i two", r=REPEATS, two=2),
+                out=pair["crossed"][:, part].rearrange("p (r i two) -> p r i two", r=REPEATS, two=2),
                 in0=acc[:].rearrange("p (r i two) -> p r i two", r=REPEATS, two=2)[:, :, :, ::-1],
                 in1=sin_table[:, tt, :]
                 .rearrange("p (i two) -> p i two", two=2)
@@ -417,20 +420,44 @@ def tile_transformerlayershard_pa_kernel(
                 .to_broadcast([P, REPEATS, ANGLES // 2, 2]),
                 op=ALU.mult,
             )
-            adder.tensor_tensor(out=turned[:], in0=straight[:], in1=crossed[:], op=ALU.add)
+
+        def add_and_store(m, c, tt, first_part, last_part, adder):
+            if first_part == 0:
+                pair["turned"] = results.tile([P, 2, CHUNK], F32, name="turned")
+            parts = slice(first_part, last_part + 1)
+            adder.tensor_tensor(
+                out=pair["turned"][:, parts].rearrange("p b n -> p (b n)"),
+                in0=pair["straight"][:, parts].rearrange("p b n -> p (b n)"),
+                in1=pair["crossed"][:, parts].rearrange("p b n -> p (b n)"),
+                op=ALU.add,
+            )
+            for part in range(first_part, last_part + 1):
+                nc.sync.dma_start(
+                    out=out_rows[m][
+                        (tt + part) * P : (tt + part + 1) * P, c * CHUNK : (c + 1) * CHUNK
+                    ],
+                    in_=pair["turned"][:, part],
+                )
 
         def finish(index):
             m, c, tt = jobs[index]
             acc = banks[(m, c, tt)]
-            rows = out_rows[m][tt * P : (tt + 1) * P, c * CHUNK : (c + 1) * CHUNK]
             if m < 2:
-                turned = results.tile([P, CHUNK], F32, name="turned")
-                rope(acc, tt, turned, nc.vector if index == last_rope_job else nc.gpsimd)
-                nc.sync.dma_start(out=rows, in_=turned[:])
+                part = tt % 2
+                rope(acc, tt, part)
+                if index == last_rope_job:
+                    add_and_store(m, c, tt - 1, 1, 1, nc.vector)
+                elif (m, c, tt + 1) == jobs[last_rope_job]:
+                    add_and_store(m, c, tt, 0, 0, nc.gpsimd)
+                elif part == 1:
+                    add_and_store(m, c, tt - 1, 0, 1, nc.gpsimd)
             else:
-                plain = results.tile([P, CHUNK], F32, name="plain")
+                plain = plain_results.tile([P, CHUNK], F32, name="plain")
                 nc.scalar.copy(out=plain[:], in_=acc[:])
-                nc.scalar.dma_start(out=rows, in_=plain[:])
+                nc.scalar.dma_start(
+                    out=out_rows[m][tt * P : (tt + 1) * P, c * CHUNK : (c + 1) * CHUNK],
+                    in_=plain[:],
+                )
 
         quantised = 3
         turned_banks = 0
@@ -450,7 +477,7 @@ def tile_transformerlayershard_pa_kernel(
                     copy_piece(halves[halves_after[index]][0])
             finish(index)
             if jobs[index][0] < 2:
-                if turned_banks % QUANTISE_EVERY == 0 and quantised < len(pieces):
+                if turned_banks in (0, 3, 5, 7, 9):
                     for piece in range(quantised, quantised + 2 - quantised % 2):
                         quantise_weight_piece(piece)
                     quantised += 2 - quantised % 2

@@ -36,7 +36,7 @@ TWO_PI_LOW = 2.0 * math.pi - TWO_PI_HIGH
 PI_BELOW = 3.1415925
 
 LOOKAHEAD = 3
-VECTOR_PIECES = 2
+VECTOR_BANKS = 2
 TENSOR_PIECES = (4, 6, 8, 10)
 HALF = CHUNK // 2
 
@@ -171,36 +171,28 @@ def tile_transformerlayershard_pa_kernel(
                 op1=ALU.max,
             )
 
-        small_steps = [
-            count_turns,
-            round_turns,
-            lambda: take_off_turns(TWO_PI_HIGH),
-            lambda: take_off_turns(TWO_PI_LOW),
-            clamp_phase,
-            absolute_phase,
-            lambda: nc.vector.tensor_copy(out=gain[:], in_=gain_bf[:].rearrange("p g t -> p (g t)")),
-            lambda: nc.vector.tensor_copy(
-                out=offset[:], in_=offset_bf[:].rearrange("p g t -> p (g t)")
-            ),
-        ]
-
         w_grouped = {}
         w_codes = {}
         w_scales = {}
 
-        def regroup_weight_piece(index):
+        def grouped_tile(index):
+            if pieces[index] not in w_grouped:
+                w_grouped[pieces[index]] = resident.tile(
+                    [P, CHUNK, PACK], BF16, name="w_grouped%d_%d_%d" % pieces[index], align_bytes=64
+                )
+            return w_grouped[pieces[index]]
+
+        def regroup_weight_columns(copy, index, first, last):
             m, c, g = pieces[index]
-            copy = nc.vector.tensor_copy if index < VECTOR_PIECES else nc.scalar.copy
-            grouped = resident.tile(
-                [P, CHUNK, PACK], BF16, name="w_grouped%d_%d_%d" % (m, c, g), align_bytes=64
-            )
             copy(
-                out=grouped[:].rearrange("p (a i) t -> p a t i", i=RUN),
-                in_=w_rows[(m, g)][:, :, c * CHUNK : (c + 1) * CHUNK].rearrange(
+                out=grouped_tile(index)[:, first:last].rearrange("p (a i) t -> p a t i", i=RUN),
+                in_=w_rows[(m, g)][:, :, c * CHUNK + first : c * CHUNK + last].rearrange(
                     "p t (a i) -> p a t i", i=RUN
                 ),
             )
-            w_grouped[(m, c, g)] = grouped
+
+        def regroup_weight_piece(index):
+            regroup_weight_columns(nc.scalar.copy, index, 0, CHUNK)
 
         def quantise_weight_piece(index):
             m, c, g = pieces[index]
@@ -234,25 +226,30 @@ def tile_transformerlayershard_pa_kernel(
             mean_var.append(small.tile([P, 2], F32, name="mean_var"))
             nc.vector.bn_aggr(out=mean_var[tt][:], in_=stats[tt][:].rearrange("p a b -> p (a b)"))
 
-        def scale_and_shift(tt):
+        def scale(tt):
             var_eps = small.tile([P, 1], F32, name="var_eps")
             nc.vector.tensor_scalar_add(out=var_eps[:], in0=mean_var[tt][:, 1:2], scalar1=EPS)
-            minus_mean = small.tile([P, 1], F32, name="minus_mean")
-            nc.vector.tensor_scalar_mul(out=minus_mean[:], in0=mean_var[tt][:, 0:1], scalar1=-1.0)
             rstd.append(small.tile([P, 1], F32, name="rstd"))
             nc.gpsimd.tensor_tensor(out=rstd[tt][:], in0=var_eps[:], in1=minus_half[:], op=ALU.pow)
+
+        def scale_and_shift(tt):
+            scale(tt)
+            minus_mean = small.tile([P, 1], F32, name="minus_mean")
+            nc.vector.tensor_scalar_mul(out=minus_mean[:], in0=mean_var[tt][:, 0:1], scalar1=-1.0)
             shift.append(small.tile([P, 1], F32, name="shift"))
             nc.gpsimd.tensor_tensor(out=shift[tt][:], in0=minus_mean[:], in1=rstd[tt][:], op=ALU.mult)
 
-        for tt in range(TOKEN_TILES):
+        measure(0, 0)
+        measure(0, 1)
+        for tt in range(1, TOKEN_TILES):
             measure(tt, 0)
-            if tt > 0:
-                scale_and_shift(tt - 1)
-            small_steps[2 * tt]()
+            aggregate(tt - 1)
             measure(tt, 1)
-            small_steps[2 * tt + 1]()
-            aggregate(tt)
-        scale_and_shift(TOKEN_TILES - 1)
+            scale_and_shift(tt - 1)
+        nc.vector.tensor_copy(out=gain[:], in_=gain_bf[:].rearrange("p g t -> p (g t)"))
+        aggregate(TOKEN_TILES - 1)
+        nc.vector.tensor_copy(out=offset[:], in_=offset_bf[:].rearrange("p g t -> p (g t)"))
+        scale(TOKEN_TILES - 1)
 
         planes = resident.tile([P, PASSES, PACK, TOKENS], BF16, name="planes")
         x_grouped = resident.tile([P, PASSES, TOKENS, PACK], BF16, name="x_grouped", align_bytes=64)
@@ -264,37 +261,52 @@ def tile_transformerlayershard_pa_kernel(
             for g in range(PASSES):
                 for t in range(PACK):
                     z_t[(g, t)] = transposed.tile([P, TOKENS], F32, name="z_t%d_%d" % (g, t))
-            for tt in range(TOKEN_TILES):
-                z = norm.tile([P, PASSES, PACK, P], F32, name="z")
-                x_sorted = x_tiles[tt][:].rearrange("q (g c t) -> q g t c", g=PASSES, t=PACK)
-                for g in range(PASSES):
-                    nc.scalar.activation(
-                        out=z[:, g],
-                        in_=x_sorted[:, g],
-                        func=ACT.Identity,
-                        scale=rstd[tt][:, 0:1],
-                        bias=shift[tt][:, 0:1],
+            z = [norm.tile([P, PASSES, PACK, P], F32, name="z") for tt in range(TOKEN_TILES)]
+
+            def x_sorted(tt, g):
+                return x_tiles[tt][:].rearrange("q (g c t) -> q g t c", g=PASSES, t=PACK)[:, g]
+
+            def normalise_on_scalar(tt, g):
+                nc.scalar.activation(
+                    out=z[tt][:, g],
+                    in_=x_sorted(tt, g),
+                    func=ACT.Identity,
+                    scale=rstd[tt][:, 0:1],
+                    bias=shift[tt][:, 0:1],
+                )
+
+            def normalise_on_vector(tt, g):
+                nc.vector.tensor_scalar(
+                    out=z[tt][:, g],
+                    in0=x_sorted(tt, g),
+                    scalar1=mean_var[tt][:, 0:1],
+                    scalar2=rstd[tt][:, 0:1],
+                    op0=ALU.subtract,
+                    op1=ALU.mult,
+                )
+
+            def transpose(tt, g):
+                for t in range(PACK):
+                    nc.tensor.transpose(
+                        z_t[(g, t)][:, tt * P : (tt + 1) * P], z[tt][:, g, t, :], identity[:]
                     )
-                    for t in range(PACK):
-                        nc.tensor.transpose(
-                            z_t[(g, t)][:, tt * P : (tt + 1) * P], z[:, g, t, :], identity[:]
-                        )
-            nc.scalar.activation(
-                out=sin_table[:].rearrange("p b c -> p (b c)"), in_=phase_flat, func=ACT.Sin
-            )
-            nc.scalar.activation(
-                out=cos_table[:].rearrange("p b c -> p (b c)"),
-                in_=turns_flat,
-                func=ACT.Sin,
-                scale=-1.0,
-                bias=0.5 * math.pi,
-            )
 
-            regroup_weight_piece(0)
-            regroup_weight_piece(1)
-            quantise_weight_piece(0)
+            for tt, g in ((0, 0), (0, 1), (1, 0), (1, 1), (2, 0)):
+                normalise_on_scalar(tt, g)
+                transpose(tt, g)
+            regroup_weight_columns(nc.scalar.copy, 0, 0, HALF)
+            count_turns()
+            normalise_on_vector(2, 1)
+            transpose(2, 1)
+            round_turns()
+            for g in range(PASSES):
+                normalise_on_vector(3, g)
+                transpose(3, g)
+            take_off_turns(TWO_PI_HIGH)
+            regroup_weight_columns(nc.vector.tensor_copy, 0, HALF, CHUNK)
+            take_off_turns(TWO_PI_LOW)
 
-            for t in range(PACK):
+            for t in range(VECTOR_BANKS):
                 nc.vector.tensor_scalar(
                     out=planes[:, 0, t, :],
                     in0=z_t[(0, t)][:],
@@ -303,14 +315,38 @@ def tile_transformerlayershard_pa_kernel(
                     op0=ALU.mult,
                     op1=ALU.add,
                 )
-                nc.scalar.activation(
-                    out=planes[:, 1, t, :],
-                    in_=z_t[(1, t)][:],
-                    func=ACT.Identity,
-                    scale=gain[:, PACK + t : PACK + t + 1],
-                    bias=offset[:, PACK + t : PACK + t + 1],
-                )
-        quantise_weight_piece(1)
+            for g in range(PASSES):
+                for t in range(VECTOR_BANKS if g == 0 else 0, PACK):
+                    nc.scalar.activation(
+                        out=planes[:, g, t, :],
+                        in_=z_t[(g, t)][:],
+                        func=ACT.Identity,
+                        scale=gain[:, g * PACK + t : g * PACK + t + 1],
+                        bias=offset[:, g * PACK + t : g * PACK + t + 1],
+                    )
+        clamp_phase()
+
+        def group_x(g):
+            nc.vector.tensor_copy(
+                out=x_grouped[:, g].rearrange("p (a i) t -> p a t i", i=RUN),
+                in_=planes[:, g].rearrange("p t (a i) -> p a t i", i=RUN),
+            )
+
+        group_x(0)
+        absolute_phase()
+        nc.scalar.activation(
+            out=sin_table[:].rearrange("p b c -> p (b c)"), in_=phase_flat, func=ACT.Sin
+        )
+        nc.scalar.activation(
+            out=cos_table[:].rearrange("p b c -> p (b c)"),
+            in_=turns_flat,
+            func=ACT.Sin,
+            scale=-1.0,
+            bias=0.5 * math.pi,
+        )
+        regroup_weight_piece(1)
+        quantise_weight_piece(0)
+        group_x(1)
 
         rope_banks = stack.enter_context(
             tc.psum_pool(name="rope_banks", bufs=LOOKAHEAD + 1, reuse_waits="tile")
@@ -341,12 +377,8 @@ def tile_transformerlayershard_pa_kernel(
 
         def copy_half(number):
             index, half = halves[number]
-            if half == 0:
-                w_grouped[pieces[index]] = resident.tile(
-                    [P, CHUNK, PACK], BF16, name="w_grouped%d_%d_%d" % pieces[index], align_bytes=64
-                )
             nc.scalar.copy(
-                out=w_grouped[pieces[index]][:, half * HALF : (half + 1) * HALF, :].rearrange(
+                out=grouped_tile(index)[:, half * HALF : (half + 1) * HALF, :].rearrange(
                     "p n t -> p (n t)"
                 ),
                 in_=half_banks[number][:],
@@ -365,18 +397,13 @@ def tile_transformerlayershard_pa_kernel(
         copy_piece(4)
 
         for g in range(PASSES):
-            nc.vector.tensor_copy(
-                out=x_grouped[:, g].rearrange("p (a i) t -> p a t i", i=RUN),
-                in_=planes[:, g].rearrange("p t (a i) -> p a t i", i=RUN),
-            )
-        for g in range(PASSES):
             nc.vector.quantize_mx(
                 out=x_codes[:, g, :].bitcast(FP8X4),
                 scales=x_scales[:, g, :],
                 in_=x_grouped[:, g].rearrange("p r t -> p (r t)"),
             )
 
-        quantise_weight_piece(2)
+        quantise_weight_piece(1)
 
         jobs = [(0, c, tt) for c in range(CHUNKS) for tt in range(TOKEN_TILES)] + [
             (m, c, tt) for c in range(CHUNKS) for tt in range(TOKEN_TILES) for m in (1, 2)
@@ -459,7 +486,7 @@ def tile_transformerlayershard_pa_kernel(
                     in_=plain[:],
                 )
 
-        quantised = 3
+        quantised = 2
         turned_banks = 0
         for m, c, tt in jobs[:LOOKAHEAD]:
             multiply(m, c, tt)

@@ -35,9 +35,14 @@ TWO_PI_HIGH = 6.28125
 TWO_PI_LOW = 2.0 * math.pi - TWO_PI_HIGH
 PI_BELOW = 3.1415925
 
-LOOKAHEAD = 3
+V_JOBS_BEFORE = (0, 0, 1, 2, 3, 4, 5, 6, 8)
+LOOKAHEAD = 2
+SCALAR_TILES = 2
 VECTOR_BANKS = 2
-TENSOR_PIECES = (4, 6, 8, 10)
+QUANTISE_BEHIND = (1, 5, 7, 9, 11)
+HALVES_AFTER = {0: 3, 2: 4, 3: 5, 5: 6, 6: 7}
+SCALAR_PIECES_AFTER = {0: (4, 7), 3: (6, 8), 6: (9, 10, 11)}
+TENSOR_PIECES = (1, 4, 6, 9)
 HALF = CHUNK // 2
 
 FLOPS = 2 * TOKENS * D * 3 * E
@@ -65,7 +70,12 @@ def tile_transformerlayershard_pa_kernel(
         x_tiles = []
         for tt in range(TOKEN_TILES):
             x_tile = resident.tile([P, D], BF16, name="x_tile%d" % tt)
-            nc.sync.dma_start(out=x_tile[:], in_=x_rows[tt * P : (tt + 1) * P, :])
+            parts = 2 if tt == 0 else 1
+            for part in range(parts):
+                columns = slice(part * D // parts, (part + 1) * D // parts)
+                nc.sync.dma_start(
+                    out=x_tile[:, columns], in_=x_rows[tt * P : (tt + 1) * P, columns]
+                )
             x_tiles.append(x_tile)
 
         gain_bf = resident.tile([P, PASSES, PACK], BF16, name="gain_bf")
@@ -110,10 +120,10 @@ def tile_transformerlayershard_pa_kernel(
         nc.vector.memset(signed_freq[:, 0:1], -1.0)
         for doubling in range(6):
             width = 2**doubling
-            nc.vector.tensor_scalar_mul(
+            nc.scalar.mul(
                 out=signed_freq[:, width : 2 * width],
-                in0=signed_freq[:, 0:width],
-                scalar1=(-FREQ_RATIO) ** width,
+                in_=signed_freq[:, 0:width],
+                mul=(-FREQ_RATIO) ** width,
             )
         phase = resident.tile([P, TOKEN_TILES, ANGLES], F32, name="phase")
         turns = resident.tile([P, TOKEN_TILES, ANGLES], F32, name="turns")
@@ -122,24 +132,23 @@ def tile_transformerlayershard_pa_kernel(
         phase_flat = phase[:].rearrange("p b c -> p (b c)")
         turns_flat = turns[:].rearrange("p b c -> p (b c)")
         for tt in range(TOKEN_TILES):
-            nc.vector.tensor_scalar_mul(
-                out=phase[:, tt, :], in0=signed_freq[:], scalar1=position[:, tt : tt + 1]
+            nc.scalar.activation(
+                out=phase[:, tt, :],
+                in_=signed_freq[:],
+                func=ACT.Copy,
+                scale=position[:, tt : tt + 1],
             )
         gain = resident.tile([P, PASSES * PACK], F32, name="gain")
         offset = resident.tile([P, PASSES * PACK], F32, name="offset")
 
-        def count_turns():
-            nc.vector.tensor_scalar(
-                out=turns_flat,
-                in0=phase_flat,
-                scalar1=0.5 / math.pi,
-                scalar2=ROUND_MAGIC,
-                op0=ALU.mult,
-                op1=ALU.add,
-            )
-
-        def round_turns():
-            nc.vector.tensor_scalar_sub(out=turns_flat, in0=turns_flat, scalar1=ROUND_MAGIC)
+        nc.scalar.activation(
+            out=turns_flat,
+            in_=phase_flat,
+            func=ACT.Copy,
+            scale=0.5 / math.pi,
+            bias=ROUND_MAGIC,
+        )
+        nc.scalar.activation(out=turns_flat, in_=turns_flat, func=ACT.Copy, bias=-ROUND_MAGIC)
 
         def take_off_turns(part_of_two_pi):
             nc.vector.scalar_tensor_tensor(
@@ -175,17 +184,18 @@ def tile_transformerlayershard_pa_kernel(
         w_codes = {}
         w_scales = {}
 
-        def grouped_tile(index):
-            if pieces[index] not in w_grouped:
-                w_grouped[pieces[index]] = resident.tile(
-                    [P, CHUNK, PACK], BF16, name="w_grouped%d_%d_%d" % pieces[index], align_bytes=64
+        def grouped_piece(index):
+            m, c, g = pieces[index]
+            if (m, c) not in w_grouped:
+                w_grouped[(m, c)] = resident.tile(
+                    [P, PASSES, CHUNK, PACK], BF16, name="w_grouped%d_%d" % (m, c), align_bytes=64
                 )
-            return w_grouped[pieces[index]]
+            return w_grouped[(m, c)][:, g]
 
         def regroup_weight_columns(copy, index, first, last):
             m, c, g = pieces[index]
             copy(
-                out=grouped_tile(index)[:, first:last].rearrange("p (a i) t -> p a t i", i=RUN),
+                out=grouped_piece(index)[:, first:last].rearrange("p (a i) t -> p a t i", i=RUN),
                 in_=w_rows[(m, g)][:, :, c * CHUNK + first : c * CHUNK + last].rearrange(
                     "p t (a i) -> p a t i", i=RUN
                 ),
@@ -194,19 +204,19 @@ def tile_transformerlayershard_pa_kernel(
         def regroup_weight_piece(index):
             regroup_weight_columns(nc.scalar.copy, index, 0, CHUNK)
 
-        def quantise_weight_piece(index):
-            m, c, g = pieces[index]
-            if g == 0:
+        def quantise_weight(m, c, first_pass, last_pass):
+            if (m, c) not in w_codes:
                 w_codes[(m, c)] = resident.tile(
                     [P, PASSES, CHUNK], U32, name="w_codes%d_%d" % (m, c), align_bytes=64
                 )
                 w_scales[(m, c)] = resident.tile(
                     [P, PASSES, CHUNK], U8, name="w_scales%d_%d" % (m, c), align_bytes=64
                 )
+            passes = slice(first_pass, last_pass + 1)
             nc.vector.quantize_mx(
-                out=w_codes[(m, c)][:, g, :].bitcast(FP8X4),
-                scales=w_scales[(m, c)][:, g, :],
-                in_=w_grouped[(m, c, g)][:].rearrange("p n t -> p (n t)"),
+                out=w_codes[(m, c)][:, passes].rearrange("p g n -> p (g n)").bitcast(FP8X4),
+                scales=w_scales[(m, c)][:, passes].rearrange("p g n -> p (g n)"),
+                in_=w_grouped[(m, c)][:, passes].rearrange("p g n t -> p (g n t)"),
             )
 
         stats = []
@@ -245,7 +255,10 @@ def tile_transformerlayershard_pa_kernel(
             measure(tt, 0)
             aggregate(tt - 1)
             measure(tt, 1)
-            scale_and_shift(tt - 1)
+            if tt - 1 < SCALAR_TILES:
+                scale_and_shift(tt - 1)
+            else:
+                scale(tt - 1)
         nc.vector.tensor_copy(out=gain[:], in_=gain_bf[:].rearrange("p g t -> p (g t)"))
         aggregate(TOKEN_TILES - 1)
         nc.vector.tensor_copy(out=offset[:], in_=offset_bf[:].rearrange("p g t -> p (g t)"))
@@ -291,19 +304,16 @@ def tile_transformerlayershard_pa_kernel(
                         z_t[(g, t)][:, tt * P : (tt + 1) * P], z[tt][:, g, t, :], identity[:]
                     )
 
-            for tt, g in ((0, 0), (0, 1), (1, 0), (1, 1), (2, 0)):
-                normalise_on_scalar(tt, g)
-                transpose(tt, g)
-            regroup_weight_columns(nc.scalar.copy, 0, 0, HALF)
-            count_turns()
-            normalise_on_vector(2, 1)
-            transpose(2, 1)
-            round_turns()
-            for g in range(PASSES):
-                normalise_on_vector(3, g)
-                transpose(3, g)
+            for tt in range(SCALAR_TILES):
+                for g in range(PASSES):
+                    normalise_on_scalar(tt, g)
+                    transpose(tt, g)
+            regroup_weight_piece(0)
+            for tt in range(SCALAR_TILES, TOKEN_TILES):
+                for g in range(PASSES):
+                    normalise_on_vector(tt, g)
+                    transpose(tt, g)
             take_off_turns(TWO_PI_HIGH)
-            regroup_weight_columns(nc.vector.tensor_copy, 0, HALF, CHUNK)
             take_off_turns(TWO_PI_LOW)
 
             for t in range(VECTOR_BANKS):
@@ -324,7 +334,6 @@ def tile_transformerlayershard_pa_kernel(
                         scale=gain[:, g * PACK + t : g * PACK + t + 1],
                         bias=offset[:, g * PACK + t : g * PACK + t + 1],
                     )
-        clamp_phase()
 
         def group_x(g):
             nc.vector.tensor_copy(
@@ -332,6 +341,8 @@ def tile_transformerlayershard_pa_kernel(
                 in_=planes[:, g].rearrange("p t (a i) -> p a t i", i=RUN),
             )
 
+        quantise_weight(0, 0, 0, 0)
+        clamp_phase()
         group_x(0)
         absolute_phase()
         nc.scalar.activation(
@@ -344,10 +355,11 @@ def tile_transformerlayershard_pa_kernel(
             scale=-1.0,
             bias=0.5 * math.pi,
         )
-        regroup_weight_piece(1)
-        quantise_weight_piece(0)
         group_x(1)
 
+        weight_banks = stack.enter_context(
+            tc.psum_pool(name="weight_banks", bufs=2, reuse_waits="tile")
+        )
         rope_banks = stack.enter_context(
             tc.psum_pool(name="rope_banks", bufs=LOOKAHEAD + 1, reuse_waits="tile")
         )
@@ -361,7 +373,7 @@ def tile_transformerlayershard_pa_kernel(
         def regroup_half(number):
             index, half = halves[number]
             m, c, g = pieces[index]
-            bank = plain_banks.tile([P, HALF * PACK], BF16, name="acc")
+            bank = weight_banks.tile([P, HALF * PACK], BF16, name="bank")
             for part in range(2):
                 first = c * CHUNK + half * HALF + part * P
                 nc.tensor.matmul(
@@ -378,7 +390,7 @@ def tile_transformerlayershard_pa_kernel(
         def copy_half(number):
             index, half = halves[number]
             nc.scalar.copy(
-                out=grouped_tile(index)[:, half * HALF : (half + 1) * HALF, :].rearrange(
+                out=grouped_piece(index)[:, half * HALF : (half + 1) * HALF, :].rearrange(
                     "p n t -> p (n t)"
                 ),
                 in_=half_banks[number][:],
@@ -388,13 +400,14 @@ def tile_transformerlayershard_pa_kernel(
             first = 2 * TENSOR_PIECES.index(index)
             copy_half(first)
             copy_half(first + 1)
-            regroup_weight_piece(index + 1)
 
         regroup_half(0)
         regroup_half(1)
-        regroup_weight_piece(2)
+        copy_piece(1)
+        regroup_half(2)
+        regroup_weight_columns(nc.scalar.copy, 2, HALF, CHUNK)
         regroup_weight_piece(3)
-        copy_piece(4)
+        regroup_weight_piece(5)
 
         for g in range(PASSES):
             nc.vector.quantize_mx(
@@ -403,11 +416,15 @@ def tile_transformerlayershard_pa_kernel(
                 in_=x_grouped[:, g].rearrange("p r t -> p (r t)"),
             )
 
-        quantise_weight_piece(1)
+        quantise_weight(0, 0, 1, 1)
+        regroup_weight_columns(nc.vector.tensor_copy, 2, 0, HALF)
 
-        jobs = [(0, c, tt) for c in range(CHUNKS) for tt in range(TOKEN_TILES)] + [
-            (m, c, tt) for c in range(CHUNKS) for tt in range(TOKEN_TILES) for m in (1, 2)
-        ]
+        jobs = [(0, c, tt) for c in range(CHUNKS) for tt in range(TOKEN_TILES)]
+        k_jobs = [(1, c, tt) for c in range(CHUNKS) for tt in range(TOKEN_TILES)]
+        v_jobs = [(2, c, tt) for c in range(CHUNKS) for tt in range(TOKEN_TILES)]
+        for number, k_job in enumerate(k_jobs):
+            jobs.append(k_job)
+            jobs.extend(v_jobs[V_JOBS_BEFORE[number] : V_JOBS_BEFORE[number + 1]])
         last_rope_job = max(index for index in range(len(jobs)) if jobs[index][0] < 2)
         banks = {}
 
@@ -473,39 +490,47 @@ def tile_transformerlayershard_pa_kernel(
                 part = tt % 2
                 rope(acc, tt, part)
                 if index == last_rope_job:
+                    add_and_store(m, c, tt - 1, 0, 0, nc.vector)
                     add_and_store(m, c, tt - 1, 1, 1, nc.vector)
-                elif (m, c, tt + 1) == jobs[last_rope_job]:
-                    add_and_store(m, c, tt, 0, 0, nc.gpsimd)
                 elif part == 1:
                     add_and_store(m, c, tt - 1, 0, 1, nc.gpsimd)
             else:
                 plain = plain_results.tile([P, CHUNK], F32, name="plain")
                 nc.scalar.copy(out=plain[:], in_=acc[:])
+                store_plain()
+                unstored.append((plain, m, c, tt))
+
+        unstored = []
+
+        def store_plain():
+            while unstored:
+                plain, m, c, tt = unstored.pop()
                 nc.scalar.dma_start(
                     out=out_rows[m][tt * P : (tt + 1) * P, c * CHUNK : (c + 1) * CHUNK],
                     in_=plain[:],
                 )
 
-        quantised = 2
+        quantised = 1
         turned_banks = 0
         for m, c, tt in jobs[:LOOKAHEAD]:
             multiply(m, c, tt)
-        regroup_half(2)
-        regroup_half(3)
-        copy_piece(6)
-        halves_after = {0: 4, 1: 5, 3: 6, 4: 7}
+        halves_after = HALVES_AFTER
         for index in range(len(jobs)):
             if index + LOOKAHEAD < len(jobs):
                 m, c, tt = jobs[index + LOOKAHEAD]
                 multiply(m, c, tt)
             if index in halves_after:
                 regroup_half(halves_after[index])
-                if halves_after[index] % 2 == 1:
-                    copy_piece(halves[halves_after[index]][0])
+            for piece in SCALAR_PIECES_AFTER.get(index, ()):
+                if piece in TENSOR_PIECES:
+                    copy_piece(piece)
+                else:
+                    regroup_weight_piece(piece)
             finish(index)
             if jobs[index][0] < 2:
-                if turned_banks in (0, 3, 5, 7, 9):
-                    for piece in range(quantised, quantised + 2 - quantised % 2):
-                        quantise_weight_piece(piece)
-                    quantised += 2 - quantised % 2
+                if turned_banks in QUANTISE_BEHIND:
+                    m, c = chunks[quantised]
+                    quantise_weight(m, c, 0, PASSES - 1)
+                    quantised += 1
                 turned_banks += 1
+        store_plain()

@@ -35,13 +35,22 @@ TWO_PI_HIGH = 6.28125
 TWO_PI_LOW = 2.0 * math.pi - TWO_PI_HIGH
 PI_BELOW = 3.1415925
 
-V_JOBS_BEFORE = (0, 0, 1, 2, 3, 4, 5, 6, 8)
 LOOKAHEAD = 2
 SCALAR_TILES = 2
 VECTOR_BANKS = 2
 QUANTISE_BEHIND = (1, 5, 7, 9, 11)
+CHUNK_ORDER = [(0, 0), (0, 1), (1, 0), (2, 0), (2, 1), (1, 1)]
+PLAIN_BUFS = 8
+FRAC_EARLY = True
+EARLY_TWO = True
+LAST_HALVES = True
+VECTOR_PAIRS = (11,)
 HALVES_AFTER = {0: 3, 2: 4, 3: 5, 5: 6, 6: 7}
-SCALAR_PIECES_AFTER = {0: (4, 7), 3: (6, 8), 6: (9, 10, 11)}
+SCALAR_WORK = {0: (4, 7), 3: (6, 8), 6: (9, 10), 8: ((0, 0), (0, 1), 11), 9: ((0, 2),), 10: ((0, 3), (1, 0)), 11: ((1, 1), (1, 2), (1, 3))}
+V_PRODUCTS = {8: ((0, 0), (0, 1)), 9: ((0, 2),), 10: ((0, 3), (1, 0)), 11: ((1, 1), (1, 2), (1, 3))}
+FLUSH_FROM = 13
+SINGLE_FROM = 12
+X_TOKENS = 256
 TENSOR_PIECES = (1, 4, 6, 9)
 HALF = CHUNK // 2
 
@@ -55,7 +64,7 @@ def tile_transformerlayershard_pa_kernel(
     weights = (Wq, Wk, Wv)
     out_rows = [o.rearrange("s h d -> s (h d)") for o in (out_0, out_1, out_2)]
     x_rows = x.rearrange("b s d -> (b s) d")
-    chunks = [(0, c) for c in range(CHUNKS)] + [(m, c) for c in range(CHUNKS) for m in (1, 2)]
+    chunks = CHUNK_ORDER
     pieces = [(m, c, g) for m, c in chunks for g in range(PASSES)]
 
     with ExitStack() as stack:
@@ -65,7 +74,7 @@ def tile_transformerlayershard_pa_kernel(
         norm = stack.enter_context(tc.tile_pool(name="norm", bufs=4))
         work = stack.enter_context(tc.tile_pool(name="work", bufs=3))
         results = stack.enter_context(tc.tile_pool(name="results", bufs=3))
-        plain_results = stack.enter_context(tc.tile_pool(name="plain_results", bufs=4))
+        plain_results = stack.enter_context(tc.tile_pool(name="plain_results", bufs=PLAIN_BUFS))
 
         x_tiles = []
         for tt in range(TOKEN_TILES):
@@ -118,12 +127,18 @@ def tile_transformerlayershard_pa_kernel(
         nc.scalar.activation(out=table_warmer[:], in_=minus_half[:], func=ACT.Sin)
         signed_freq = resident.tile([P, ANGLES], F32, name="signed_freq")
         nc.vector.memset(signed_freq[:, 0:1], -1.0)
-        for doubling in range(6):
+        for column in range(1, 4):
+            nc.vector.tensor_scalar_mul(
+                out=signed_freq[:, column : column + 1],
+                in0=signed_freq[:, 0:1],
+                scalar1=(-FREQ_RATIO) ** column,
+            )
+        for doubling in range(2, 6):
             width = 2**doubling
-            nc.scalar.mul(
+            nc.vector.tensor_scalar_mul(
                 out=signed_freq[:, width : 2 * width],
-                in_=signed_freq[:, 0:width],
-                mul=(-FREQ_RATIO) ** width,
+                in0=signed_freq[:, 0:width],
+                scalar1=(-FREQ_RATIO) ** width,
             )
         phase = resident.tile([P, TOKEN_TILES, ANGLES], F32, name="phase")
         turns = resident.tile([P, TOKEN_TILES, ANGLES], F32, name="turns")
@@ -150,24 +165,14 @@ def tile_transformerlayershard_pa_kernel(
         )
         nc.scalar.activation(out=turns_flat, in_=turns_flat, func=ACT.Copy, bias=-ROUND_MAGIC)
 
-        def take_off_turns(part_of_two_pi):
+        def take_off_turns():
             nc.vector.scalar_tensor_tensor(
                 out=phase_flat,
-                in0=turns_flat,
-                scalar=-part_of_two_pi,
-                in1=phase_flat,
-                op0=ALU.mult,
-                op1=ALU.add,
-            )
-
-        def clamp_phase():
-            nc.vector.tensor_scalar(
-                out=phase_flat,
                 in0=phase_flat,
-                scalar1=PI_BELOW,
-                scalar2=-PI_BELOW,
-                op0=ALU.min,
-                op1=ALU.max,
+                scalar=0.5 / math.pi,
+                in1=turns_flat,
+                op0=ALU.mult,
+                op1=ALU.subtract,
             )
 
         def absolute_phase():
@@ -259,10 +264,12 @@ def tile_transformerlayershard_pa_kernel(
                 scale_and_shift(tt - 1)
             else:
                 scale(tt - 1)
-        nc.vector.tensor_copy(out=gain[:], in_=gain_bf[:].rearrange("p g t -> p (g t)"))
         aggregate(TOKEN_TILES - 1)
-        nc.vector.tensor_copy(out=offset[:], in_=offset_bf[:].rearrange("p g t -> p (g t)"))
+        if FRAC_EARLY:
+            take_off_turns()
         scale(TOKEN_TILES - 1)
+        nc.gpsimd.tensor_copy(out=gain[:], in_=gain_bf[:].rearrange("p g t -> p (g t)"))
+        nc.gpsimd.tensor_copy(out=offset[:], in_=offset_bf[:].rearrange("p g t -> p (g t)"))
 
         planes = resident.tile([P, PASSES, PACK, TOKENS], BF16, name="planes")
         x_grouped = resident.tile([P, PASSES, TOKENS, PACK], BF16, name="x_grouped", align_bytes=64)
@@ -313,8 +320,8 @@ def tile_transformerlayershard_pa_kernel(
                 for g in range(PASSES):
                     normalise_on_vector(tt, g)
                     transpose(tt, g)
-            take_off_turns(TWO_PI_HIGH)
-            take_off_turns(TWO_PI_LOW)
+            if not FRAC_EARLY:
+                take_off_turns()
 
             for t in range(VECTOR_BANKS):
                 nc.vector.tensor_scalar(
@@ -342,19 +349,9 @@ def tile_transformerlayershard_pa_kernel(
             )
 
         quantise_weight(0, 0, 0, 0)
-        clamp_phase()
         group_x(0)
         absolute_phase()
-        nc.scalar.activation(
-            out=sin_table[:].rearrange("p b c -> p (b c)"), in_=phase_flat, func=ACT.Sin
-        )
-        nc.scalar.activation(
-            out=cos_table[:].rearrange("p b c -> p (b c)"),
-            in_=turns_flat,
-            func=ACT.Sin,
-            scale=-1.0,
-            bias=0.5 * math.pi,
-        )
+        regroup_weight_columns(nc.vector.tensor_copy, 2, 0, HALF)
         group_x(1)
 
         weight_banks = stack.enter_context(
@@ -405,32 +402,41 @@ def tile_transformerlayershard_pa_kernel(
         regroup_half(1)
         copy_piece(1)
         regroup_half(2)
+        nc.scalar.activation(
+            out=sin_table[:].rearrange("p b c -> p (b c)"), in_=phase_flat, func=ACT.Sin, scale=2.0 * math.pi
+        )
+        nc.scalar.activation(
+            out=cos_table[:].rearrange("p b c -> p (b c)"),
+            in_=turns_flat,
+            func=ACT.Sin,
+            scale=-2.0 * math.pi,
+            bias=0.5 * math.pi,
+        )
         regroup_weight_columns(nc.scalar.copy, 2, HALF, CHUNK)
         regroup_weight_piece(3)
         regroup_weight_piece(5)
 
-        for g in range(PASSES):
-            nc.vector.quantize_mx(
-                out=x_codes[:, g, :].bitcast(FP8X4),
-                scales=x_scales[:, g, :],
-                in_=x_grouped[:, g].rearrange("p r t -> p (r t)"),
-            )
-
         quantise_weight(0, 0, 1, 1)
-        regroup_weight_columns(nc.vector.tensor_copy, 2, 0, HALF)
+        for first in range(0, TOKENS, X_TOKENS):
+            for g in range(PASSES):
+                nc.vector.quantize_mx(
+                    out=x_codes[:, g, first : first + X_TOKENS].bitcast(FP8X4),
+                    scales=x_scales[:, g, first : first + X_TOKENS],
+                    in_=x_grouped[:, g, first : first + X_TOKENS].rearrange("p r t -> p (r t)"),
+                )
 
-        jobs = [(0, c, tt) for c in range(CHUNKS) for tt in range(TOKEN_TILES)]
-        k_jobs = [(1, c, tt) for c in range(CHUNKS) for tt in range(TOKEN_TILES)]
-        v_jobs = [(2, c, tt) for c in range(CHUNKS) for tt in range(TOKEN_TILES)]
-        for number, k_job in enumerate(k_jobs):
-            jobs.append(k_job)
-            jobs.extend(v_jobs[V_JOBS_BEFORE[number] : V_JOBS_BEFORE[number + 1]])
-        last_rope_job = max(index for index in range(len(jobs)) if jobs[index][0] < 2)
+        if EARLY_TWO:
+            quantise_weight(0, 1, 0, 0)
+
+        rope_jobs = [(m, c, tt) for m in (0, 1) for c in range(CHUNKS) for tt in range(TOKEN_TILES)]
         banks = {}
 
         def multiply(m, c, tt):
-            pool = rope_banks if m < 2 else plain_banks
-            acc = pool.tile([P, CHUNK], F32, name="acc")
+            if m == 2 and c * TOKEN_TILES + tt in (3, 4):
+                acc = weight_banks.tile([P, CHUNK], F32, name="bank")
+            else:
+                pool = rope_banks if m < 2 else plain_banks
+                acc = pool.tile([P, CHUNK], F32, name="acc")
             for g in range(PASSES):
                 nc.tensor.matmul_mx(
                     out=acc[:],
@@ -483,54 +489,73 @@ def tile_transformerlayershard_pa_kernel(
                     in_=pair["turned"][:, part],
                 )
 
-        def finish(index):
-            m, c, tt = jobs[index]
-            acc = banks[(m, c, tt)]
-            if m < 2:
-                part = tt % 2
-                rope(acc, tt, part)
-                if index == last_rope_job:
-                    add_and_store(m, c, tt - 1, 0, 0, nc.vector)
-                    add_and_store(m, c, tt - 1, 1, 1, nc.vector)
-                elif part == 1:
-                    add_and_store(m, c, tt - 1, 0, 1, nc.gpsimd)
-            else:
-                plain = plain_results.tile([P, CHUNK], F32, name="plain")
-                nc.scalar.copy(out=plain[:], in_=acc[:])
-                store_plain()
-                unstored.append((plain, m, c, tt))
-
         unstored = []
 
         def store_plain():
             while unstored:
-                plain, m, c, tt = unstored.pop()
+                plain, c, tt = unstored.pop()
                 nc.scalar.dma_start(
-                    out=out_rows[m][tt * P : (tt + 1) * P, c * CHUNK : (c + 1) * CHUNK],
+                    out=out_rows[2][tt * P : (tt + 1) * P, c * CHUNK : (c + 1) * CHUNK],
                     in_=plain[:],
                 )
 
+        def finish_plain(c, tt):
+            plain = plain_results.tile([P, CHUNK], F32, name="plain")
+            nc.scalar.copy(out=plain[:], in_=banks[(2, c, tt)][:])
+            store_plain()
+            unstored.append((plain, c, tt))
+
         quantised = 1
-        turned_banks = 0
-        for m, c, tt in jobs[:LOOKAHEAD]:
-            multiply(m, c, tt)
-        halves_after = HALVES_AFTER
-        for index in range(len(jobs)):
-            if index + LOOKAHEAD < len(jobs):
-                m, c, tt = jobs[index + LOOKAHEAD]
-                multiply(m, c, tt)
-            if index in halves_after:
-                regroup_half(halves_after[index])
-            for piece in SCALAR_PIECES_AFTER.get(index, ()):
-                if piece in TENSOR_PIECES:
-                    copy_piece(piece)
+        multiplied = 0
+        for step in range(len(rope_jobs)):
+            while (
+                multiplied < min(step + LOOKAHEAD + 1, len(rope_jobs))
+                and rope_jobs[multiplied][:2] in chunks[:quantised]
+            ):
+                multiply(*rope_jobs[multiplied])
+                multiplied += 1
+            if step in HALVES_AFTER:
+                regroup_half(HALVES_AFTER[step])
+            for c, tt in V_PRODUCTS.get(step, ()):
+                multiply(2, c, tt)
+            for work_item in SCALAR_WORK.get(step, ()):
+                if isinstance(work_item, tuple):
+                    finish_plain(*work_item)
                 else:
-                    regroup_weight_piece(piece)
-            finish(index)
-            if jobs[index][0] < 2:
-                if turned_banks in QUANTISE_BEHIND:
-                    m, c = chunks[quantised]
-                    quantise_weight(m, c, 0, PASSES - 1)
-                    quantised += 1
-                turned_banks += 1
+                    if work_item in TENSOR_PIECES:
+                        copy_piece(work_item)
+                    else:
+                        regroup_weight_piece(work_item)
+                    store_plain()
+            if step >= FLUSH_FROM:
+                store_plain()
+            m, c, tt = rope_jobs[step]
+            part = tt % 2
+            rope(banks[(m, c, tt)], tt, part)
+            if step in QUANTISE_BEHIND:
+                quantise_weight(*chunks[quantised], 1 if quantised == 1 and EARLY_TWO else 0, PASSES - 1)
+                quantised += 1
+            if step == len(rope_jobs) - 1 or step in VECTOR_PAIRS:
+                add_and_store(m, c, tt - 1, 0, 0, nc.vector)
+                if step == len(rope_jobs) - 1 and LAST_HALVES:
+                    for first in range(0, CHUNK, CHUNK // 2):
+                        cols = slice(first, first + CHUNK // 2)
+                        nc.vector.tensor_tensor(
+                            out=pair["turned"][:, 1, cols],
+                            in0=pair["straight"][:, 1, cols],
+                            in1=pair["crossed"][:, 1, cols],
+                            op=ALU.add,
+                        )
+                        nc.sync.dma_start(
+                            out=out_rows[m][
+                                tt * P : (tt + 1) * P, c * CHUNK + first : c * CHUNK + first + CHUNK // 2
+                            ],
+                            in_=pair["turned"][:, 1, cols],
+                        )
+                else:
+                    add_and_store(m, c, tt - 1, 1, 1, nc.vector)
+            elif step >= SINGLE_FROM and step < len(rope_jobs) - 2:
+                add_and_store(m, c, tt - part, part, part, nc.gpsimd)
+            elif part == 1 :
+                add_and_store(m, c, tt - 1, 0, 1, nc.gpsimd)
         store_plain()

@@ -38,18 +38,23 @@ PI_BELOW = 3.1415925
 LOOKAHEAD = 2
 SCALAR_TILES = 2
 VECTOR_BANKS = 2
-QUANTISE_BEHIND = (1, 5, 7, 9, 11)
+QUANTISE_BEHIND = (1, 3, 5, 7, 10)
 CHUNK_ORDER = [(0, 0), (0, 1), (1, 0), (2, 0), (2, 1), (1, 1)]
 PLAIN_BUFS = 8
-FRAC_EARLY = True
+FRAC_EARLY = False
 EARLY_TWO = True
 LAST_HALVES = True
-VECTOR_PAIRS = (11,)
-HALVES_AFTER = {0: 3, 2: 4, 3: 5, 5: 6, 6: 7}
-SCALAR_WORK = {0: (4, 7), 3: (6, 8), 6: (9, 10), 8: ((0, 0), (0, 1), 11), 9: ((0, 2),), 10: ((0, 3), (1, 0)), 11: ((1, 1), (1, 2), (1, 3))}
-V_PRODUCTS = {8: ((0, 0), (0, 1)), 9: ((0, 2),), 10: ((0, 3), (1, 0)), 11: ((1, 1), (1, 2), (1, 3))}
+VECTOR_PAIRS = ()
+HALVES_AFTER = {0: (3,), 2: (4, 5), 4: (6, 7)}
+GPSIMD_COLUMNS = 256
+TWO_FIRST = True
+EARLY_HALVES = 3
+TENSOR_HALVES = [(1, 0), (1, 1), (4, 0), (4, 1), (6, 0), (6, 1), (9, 0), (9, 1)]
+SCALAR_WORK = {0: (4, 7), 3: (6, 8), 6: (9, 10, 11, (0, 0)), 7: ((0, 1),), 8: ((0, 2),), 9: ((0, 3), (1, 0)), 10: ((1, 1), (1, 2)), 11: ((1, 3),)}
+V_PRODUCTS = {6: ((0, 0),), 7: ((0, 1),), 8: ((0, 2),), 9: ((0, 3), (1, 0)), 10: ((1, 1), (1, 2)), 11: ((1, 3),)}
 FLUSH_FROM = 13
-SINGLE_FROM = 12
+SINGLE_FROM = 8
+LAST_GPSIMD = 14
 X_TOKENS = 256
 TENSOR_PIECES = (1, 4, 6, 9)
 HALF = CHUNK // 2
@@ -364,7 +369,7 @@ def tile_transformerlayershard_pa_kernel(
             tc.psum_pool(name="plain_banks", bufs=LOOKAHEAD + 1, reuse_waits="tile")
         )
 
-        halves = [(index, half) for index in TENSOR_PIECES for half in range(2)]
+        halves = TENSOR_HALVES
         half_banks = {}
 
         def regroup_half(number):
@@ -394,14 +399,14 @@ def tile_transformerlayershard_pa_kernel(
             )
 
         def copy_piece(index):
-            first = 2 * TENSOR_PIECES.index(index)
-            copy_half(first)
-            copy_half(first + 1)
+            for half in range(2):
+                copy_half(halves.index((index, half)))
 
         regroup_half(0)
         regroup_half(1)
         copy_piece(1)
-        regroup_half(2)
+        for number in range(2, EARLY_HALVES):
+            regroup_half(number)
         nc.scalar.activation(
             out=sin_table[:].rearrange("p b c -> p (b c)"), in_=phase_flat, func=ACT.Sin, scale=2.0 * math.pi
         )
@@ -412,9 +417,18 @@ def tile_transformerlayershard_pa_kernel(
             scale=-2.0 * math.pi,
             bias=0.5 * math.pi,
         )
-        regroup_weight_columns(nc.scalar.copy, 2, HALF, CHUNK)
+        def copy_two():
+            if (2, 1) in halves:
+                copy_half(halves.index((2, 1)))
+            else:
+                regroup_weight_columns(nc.scalar.copy, 2, HALF, CHUNK)
+
+        if TWO_FIRST:
+            copy_two()
         regroup_weight_piece(3)
-        regroup_weight_piece(5)
+        if not TWO_FIRST:
+            copy_two()
+        regroup_weight_columns(nc.scalar.copy, 5, GPSIMD_COLUMNS, CHUNK)
 
         quantise_weight(0, 0, 1, 1)
         for first in range(0, TOKENS, X_TOKENS):
@@ -427,6 +441,18 @@ def tile_transformerlayershard_pa_kernel(
 
         if EARLY_TWO:
             quantise_weight(0, 1, 0, 0)
+
+        fence = resident.tile([P, 1], U32, name="fence")
+        last_codes = w_codes[(0, 1)][:, 0, CHUNK - 1 : CHUNK] if EARLY_TWO else x_codes[:, PASSES - 1, TOKENS - 1 : TOKENS]
+        nc.gpsimd.tensor_copy(out=fence[:], in_=last_codes)
+
+        def regroup_on_gpsimd(out, in_):
+            nc.gpsimd.tensor_scalar(
+                out=out, in0=in_, scalar1=1.0, scalar2=0.0, op0=ALU.mult, op1=ALU.add
+            )
+
+        if GPSIMD_COLUMNS:
+            regroup_weight_columns(regroup_on_gpsimd, 5, 0, GPSIMD_COLUMNS)
 
         rope_jobs = [(m, c, tt) for m in (0, 1) for c in range(CHUNKS) for tt in range(TOKEN_TILES)]
         banks = {}
@@ -449,20 +475,26 @@ def tile_transformerlayershard_pa_kernel(
                 )
             banks[(m, c, tt)] = acc
 
-        pair = {}
+        pairs = []
 
-        def rope(acc, tt, part):
+        def rope(step):
+            m, c, tt = rope_jobs[step]
+            part = step % 2
             if part == 0:
-                pair["straight"] = work.tile([P, 2, CHUNK], F32, name="straight")
-                pair["crossed"] = work.tile([P, 2, CHUNK], F32, name="crossed")
+                straight = work.tile([P, 2, CHUNK], F32, name="straight")
+                crossed = work.tile([P, 2, CHUNK], F32, name="crossed")
+                turned = results.tile([P, 2, CHUNK], F32, name="turned")
+                pairs.append((straight, crossed, turned))
+            straight, crossed, turned = pairs[-1]
+            acc = banks[(m, c, tt)]
             nc.vector.tensor_tensor(
-                out=pair["straight"][:, part].rearrange("p (r m) -> p r m", m=ANGLES),
+                out=straight[:, part].rearrange("p (r m) -> p r m", m=ANGLES),
                 in0=acc[:].rearrange("p (r m) -> p r m", m=ANGLES),
                 in1=cos_table[:, tt, :].unsqueeze(1).to_broadcast([P, REPEATS, ANGLES]),
                 op=ALU.mult,
             )
             nc.vector.tensor_tensor(
-                out=pair["crossed"][:, part].rearrange("p (r i two) -> p r i two", r=REPEATS, two=2),
+                out=crossed[:, part].rearrange("p (r i two) -> p r i two", r=REPEATS, two=2),
                 in0=acc[:].rearrange("p (r i two) -> p r i two", r=REPEATS, two=2)[:, :, :, ::-1],
                 in1=sin_table[:, tt, :]
                 .rearrange("p (i two) -> p i two", two=2)
@@ -471,22 +503,22 @@ def tile_transformerlayershard_pa_kernel(
                 op=ALU.mult,
             )
 
-        def add_and_store(m, c, tt, first_part, last_part, adder):
-            if first_part == 0:
-                pair["turned"] = results.tile([P, 2, CHUNK], F32, name="turned")
-            parts = slice(first_part, last_part + 1)
-            adder.tensor_tensor(
-                out=pair["turned"][:, parts].rearrange("p b n -> p (b n)"),
-                in0=pair["straight"][:, parts].rearrange("p b n -> p (b n)"),
-                in1=pair["crossed"][:, parts].rearrange("p b n -> p (b n)"),
-                op=ALU.add,
+        def add(adder, step, count=1, first=0, last=CHUNK):
+            part = step % 2
+            straight, crossed, turned = (
+                tile[:, part : part + count, first:last].rearrange("p b n -> p (b n)")
+                if count == 1 or last - first == CHUNK
+                else tile[:, part : part + count, first:last]
+                for tile in pairs[step // 2]
             )
-            for part in range(first_part, last_part + 1):
+            adder.tensor_tensor(out=turned, in0=straight, in1=crossed, op=ALU.add)
+            for bank in range(step, step + count):
+                m, c, tt = rope_jobs[bank]
                 nc.sync.dma_start(
                     out=out_rows[m][
-                        (tt + part) * P : (tt + part + 1) * P, c * CHUNK : (c + 1) * CHUNK
+                        tt * P : (tt + 1) * P, c * CHUNK + first : c * CHUNK + last
                     ],
-                    in_=pair["turned"][:, part],
+                    in_=pairs[bank // 2][2][:, bank % 2, first:last],
                 )
 
         unstored = []
@@ -514,8 +546,8 @@ def tile_transformerlayershard_pa_kernel(
             ):
                 multiply(*rope_jobs[multiplied])
                 multiplied += 1
-            if step in HALVES_AFTER:
-                regroup_half(HALVES_AFTER[step])
+            for number in HALVES_AFTER.get(step, ()):
+                regroup_half(number)
             for c, tt in V_PRODUCTS.get(step, ()):
                 multiply(2, c, tt)
             for work_item in SCALAR_WORK.get(step, ()):
@@ -529,33 +561,21 @@ def tile_transformerlayershard_pa_kernel(
                     store_plain()
             if step >= FLUSH_FROM:
                 store_plain()
-            m, c, tt = rope_jobs[step]
-            part = tt % 2
-            rope(banks[(m, c, tt)], tt, part)
+            rope(step)
             if step in QUANTISE_BEHIND:
-                quantise_weight(*chunks[quantised], 1 if quantised == 1 and EARLY_TWO else 0, PASSES - 1)
+                quantise_weight(
+                    *chunks[quantised], 1 if quantised == 1 and EARLY_TWO else 0, PASSES - 1
+                )
                 quantised += 1
-            if step == len(rope_jobs) - 1 or step in VECTOR_PAIRS:
-                add_and_store(m, c, tt - 1, 0, 0, nc.vector)
-                if step == len(rope_jobs) - 1 and LAST_HALVES:
-                    for first in range(0, CHUNK, CHUNK // 2):
-                        cols = slice(first, first + CHUNK // 2)
-                        nc.vector.tensor_tensor(
-                            out=pair["turned"][:, 1, cols],
-                            in0=pair["straight"][:, 1, cols],
-                            in1=pair["crossed"][:, 1, cols],
-                            op=ALU.add,
-                        )
-                        nc.sync.dma_start(
-                            out=out_rows[m][
-                                tt * P : (tt + 1) * P, c * CHUNK + first : c * CHUNK + first + CHUNK // 2
-                            ],
-                            in_=pair["turned"][:, 1, cols],
-                        )
-                else:
-                    add_and_store(m, c, tt - 1, 1, 1, nc.vector)
-            elif step >= SINGLE_FROM and step < len(rope_jobs) - 2:
-                add_and_store(m, c, tt - part, part, part, nc.gpsimd)
-            elif part == 1 :
-                add_and_store(m, c, tt - 1, 0, 1, nc.gpsimd)
+            if step < SINGLE_FROM:
+                if step % 2 == 1:
+                    add(nc.gpsimd, step - 1, count=2)
+            elif step < LAST_GPSIMD:
+                add(nc.gpsimd, step)
+            elif step > LAST_GPSIMD and step < len(rope_jobs) - 1:
+                add(nc.vector, step - 1)
+            elif step == len(rope_jobs) - 1:
+                add(nc.vector, step - 1)
+                add(nc.vector, step, last=CHUNK // 2)
+                add(nc.vector, step, first=CHUNK // 2)
         store_plain()

@@ -46,13 +46,15 @@ EARLY_TWO = True
 LAST_HALVES = True
 VECTOR_PAIRS = ()
 HALVES_AFTER = {0: (3,), 2: (4, 5), 4: (6, 7)}
-GPSIMD_COLUMNS = 256
+GPSIMD_COLUMNS = 192
 TWO_FIRST = True
 EARLY_HALVES = 3
 TENSOR_HALVES = [(1, 0), (1, 1), (4, 0), (4, 1), (6, 0), (6, 1), (9, 0), (9, 1)]
-SCALAR_WORK = {0: (4, 7), 3: (6, 8), 6: (9, 10, 11, (0, 0)), 7: ((0, 1),), 8: ((0, 2),), 9: ((0, 3), (1, 0)), 10: ((1, 1), (1, 2)), 11: ((1, 3),)}
+SCALAR_WORK = {0: (4, 7), 3: (6, 8), 6: (9, 10, (0, 0), 11), 7: ((0, 1),), 8: ((0, 2),), 9: ((0, 3), (1, 0)), 10: ((1, 1), (1, 2)), 11: ((1, 3),)}
 V_PRODUCTS = {6: ((0, 0),), 7: ((0, 1),), 8: ((0, 2),), 9: ((0, 3), (1, 0)), 10: ((1, 1), (1, 2)), 11: ((1, 3),)}
 FLUSH_FROM = 13
+VECTOR_ADDS = {10: 9}
+VADD_FIRST = False
 SINGLE_FROM = 8
 LAST_GPSIMD = 14
 X_TOKENS = 256
@@ -446,13 +448,18 @@ def tile_transformerlayershard_pa_kernel(
         last_codes = w_codes[(0, 1)][:, 0, CHUNK - 1 : CHUNK] if EARLY_TWO else x_codes[:, PASSES - 1, TOKENS - 1 : TOKENS]
         nc.gpsimd.tensor_copy(out=fence[:], in_=last_codes)
 
-        def regroup_on_gpsimd(out, in_):
-            nc.gpsimd.tensor_scalar(
-                out=out, in0=in_, scalar1=1.0, scalar2=0.0, op0=ALU.mult, op1=ALU.add
-            )
-
         if GPSIMD_COLUMNS:
-            regroup_weight_columns(regroup_on_gpsimd, 5, 0, GPSIMD_COLUMNS)
+            m, c, g = pieces[5]
+            nc.gpsimd.tensor_scalar(
+                out=grouped_piece(5)[:, 0:GPSIMD_COLUMNS],
+                in0=w_rows[(m, g)][:, :, c * CHUNK : c * CHUNK + GPSIMD_COLUMNS].rearrange(
+                    "p t n -> p n t"
+                ),
+                scalar1=1.0,
+                scalar2=0.0,
+                op0=ALU.mult,
+                op1=ALU.add,
+            )
 
         rope_jobs = [(m, c, tt) for m in (0, 1) for c in range(CHUNKS) for tt in range(TOKEN_TILES)]
         banks = {}
@@ -557,17 +564,25 @@ def tile_transformerlayershard_pa_kernel(
                     if work_item in TENSOR_PIECES:
                         copy_piece(work_item)
                     else:
-                        regroup_weight_piece(work_item)
+                        regroup_weight_columns(nc.scalar.copy, work_item, 0, HALF)
+                        store_plain()
+                        regroup_weight_columns(nc.scalar.copy, work_item, HALF, CHUNK)
                     store_plain()
             if step >= FLUSH_FROM:
                 store_plain()
             rope(step)
+            if step in VECTOR_ADDS and VADD_FIRST:
+                add(nc.vector, VECTOR_ADDS[step])
             if step in QUANTISE_BEHIND:
                 quantise_weight(
                     *chunks[quantised], 1 if quantised == 1 and EARLY_TWO else 0, PASSES - 1
                 )
                 quantised += 1
-            if step < SINGLE_FROM:
+            if step in VECTOR_ADDS and not VADD_FIRST:
+                add(nc.vector, VECTOR_ADDS[step])
+            if step in VECTOR_ADDS.values():
+                pass
+            elif step < SINGLE_FROM:
                 if step % 2 == 1:
                     add(nc.gpsimd, step - 1, count=2)
             elif step < LAST_GPSIMD:

import math
from contextlib import ExitStack

import concourse.mybir as mybir
from concourse.masks import make_identity

F32 = mybir.dt.float32
BF16 = mybir.dt.bfloat16
U32 = mybir.dt.uint32
U8 = mybir.dt.uint8
FP8X4 = mybir.dt.float8_e4m3fn_x4
ALU = mybir.AluOpType
ACT = mybir.ActivationFunctionType

P = 128
TOKENS = 512
D = 1024
E = 1024
PACK = 4
K_PASS = P * PACK
PASSES = D // K_PASS
TOKEN_TILES = TOKENS // P
CHUNK = 512
CHUNKS = E // CHUNK
ANGLES = 64
REPEATS = CHUNK // ANGLES
RUN = 4
EPS = 1e-5
BN_STATS_MAX = 512
BN_STATS_DIM = 6

FREQ_RATIO = 10000.0 ** (-1.0 / ANGLES)
ROUND_MAGIC = 1.5 * 2.0**23
TWO_PI_HIGH = 6.28125
TWO_PI_LOW = 2.0 * math.pi - TWO_PI_HIGH
PI_BELOW = 3.1415925

LOOKAHEAD = 2
SCALAR_TILES = 2
VECTOR_BANKS = 2
QUANTISE_BEHIND = (1, 3, 5, 7, 10)
CHUNK_ORDER = [(0, 0), (0, 1), (1, 0), (2, 0), (2, 1), (1, 1)]
PLAIN_BUFS = 8
FRAC_EARLY = False
EARLY_TWO = True
LAST_HALVES = True
VECTOR_PAIRS = ()
HALVES_AFTER = {0: (3,), 2: (4, 5), 4: (6, 7)}
GPSIMD_COLUMNS = 192
TWO_FIRST = True
EARLY_HALVES = 3
TENSOR_HALVES = [(1, 0), (1, 1), (4, 0), (4, 1), (6, 0), (6, 1), (9, 0), (9, 1)]
SCALAR_WORK = {0: (4, 7), 3: (6, 8), 6: (9, 10, (0, 0), 11), 7: ((0, 1),), 8: ((0, 2),), 9: ((0, 3), (1, 0)), 10: ((1, 1), (1, 2)), 11: ((1, 3),)}
V_PRODUCTS = {6: ((0, 0),), 7: ((0, 1),), 8: ((0, 2),), 9: ((0, 3), (1, 0)), 10: ((1, 1), (1, 2)), 11: ((1, 3),)}
FLUSH_FROM = 13
VECTOR_ADDS = {10: 9}
VADD_FIRST = False
SINGLE_FROM = 8
LAST_GPSIMD = 14
X_TOKENS = 256
TENSOR_PIECES = (1, 4, 6, 9)
HALF = CHUNK // 2

FLOPS = 2 * TOKENS * D * 3 * E


def tile_transformerlayershard_pa_kernel(
    tc, x, ln_scale, ln_offset, Wq, Wk, Wv, out_0, out_1, out_2
):
    nc = tc.nc
    weights = (Wq, Wk, Wv)
    out_rows = [o.rearrange("s h d -> s (h d)") for o in (out_0, out_1, out_2)]
    x_rows = x.rearrange("b s d -> (b s) d")
    chunks = CHUNK_ORDER
    pieces = [(m, c, g) for m, c in chunks for g in range(PASSES)]

    with ExitStack() as stack:
        stack.enter_context(tc.manual_schedule())
        resident = stack.enter_context(tc.tile_pool(name="resident", bufs=1))
        small = stack.enter_context(tc.tile_pool(name="small", bufs=4))
        norm = stack.enter_context(tc.tile_pool(name="norm", bufs=4))
        work = stack.enter_context(tc.tile_pool(name="work", bufs=3))
        results = stack.enter_context(tc.tile_pool(name="results", bufs=3))
        plain_results = stack.enter_context(tc.tile_pool(name="plain_results", bufs=PLAIN_BUFS))

        x_tiles = []
        for tt in range(TOKEN_TILES):
            x_tile = resident.tile([P, D], BF16, name="x_tile%d" % tt)
            parts = 2 if tt == 0 else 1
            for part in range(parts):
                columns = slice(part * D // parts, (part + 1) * D // parts)
                nc.sync.dma_start(
                    out=x_tile[:, columns], in_=x_rows[tt * P : (tt + 1) * P, columns]
                )
            x_tiles.append(x_tile)

        gain_bf = resident.tile([P, PASSES, PACK], BF16, name="gain_bf")
        offset_bf = resident.tile([P, PASSES, PACK], BF16, name="offset_bf")
        with nc.allow_non_contiguous_dma(reason="two vectors of 1024, four values to a piece"):
            nc.sync.dma_start(
                out=gain_bf[:], in_=ln_scale.rearrange("(g p t) -> p g t", g=PASSES, t=PACK)
            )
            nc.sync.dma_start(
                out=offset_bf[:], in_=ln_offset.rearrange("(g p t) -> p g t", g=PASSES, t=PACK)
            )

        w_rows = {}
        for m in range(3):
            for g in range(PASSES):
                w_tile = resident.tile([P, PACK, E], BF16, name="w_rows%d_%d" % (m, g))
                nc.sync.dma_start(
                    out=w_tile[:],
                    in_=weights[m][g * K_PASS : (g + 1) * K_PASS, :].rearrange(
                        "(p t) n -> p t n", t=PACK
                    ),
                )
                w_rows[(m, g)] = w_tile

        position = resident.tile([P, TOKEN_TILES], F32, name="position")
        nc.gpsimd.iota(
            position[:],
            pattern=[[P, TOKEN_TILES]],
            base=0,
            channel_multiplier=1,
            allow_small_or_imprecise_dtypes=True,
        )
        identity = resident.tile([P, P], F32, name="identity")
        make_identity(nc, identity[:])
        identity_bf = resident.tile([P, P], BF16, name="identity_bf")
        nc.gpsimd.tensor_copy(out=identity_bf[:], in_=identity[:])
        minus_half = resident.tile([P, 1], F32, name="minus_half")
        nc.vector.memset(minus_half[:], -0.5)
        table_warmer = resident.tile([P, 1], F32, name="table_warmer")
        nc.scalar.activation(out=table_warmer[:], in_=minus_half[:], func=ACT.Sin)
        signed_freq = resident.tile([P, ANGLES], F32, name="signed_freq")
        nc.vector.memset(signed_freq[:, 0:1], -1.0)
        for column in range(1, 4):
            nc.vector.tensor_scalar_mul(
                out=signed_freq[:, column : column + 1],
                in0=signed_freq[:, 0:1],
                scalar1=(-FREQ_RATIO) ** column,
            )
        for doubling in range(2, 6):
            width = 2**doubling
            nc.vector.tensor_scalar_mul(
                out=signed_freq[:, width : 2 * width],
                in0=signed_freq[:, 0:width],
                scalar1=(-FREQ_RATIO) ** width,
            )
        phase = resident.tile([P, TOKEN_TILES, ANGLES], F32, name="phase")
        turns = resident.tile([P, TOKEN_TILES, ANGLES], F32, name="turns")
        cos_table = resident.tile([P, TOKEN_TILES, ANGLES], F32, name="cos_table")
        sin_table = resident.tile([P, TOKEN_TILES, ANGLES], F32, name="sin_table")
        phase_flat = phase[:].rearrange("p b c -> p (b c)")
        turns_flat = turns[:].rearrange("p b c -> p (b c)")
        for tt in range(TOKEN_TILES):
            nc.scalar.activation(
                out=phase[:, tt, :],
                in_=signed_freq[:],
                func=ACT.Copy,
                scale=position[:, tt : tt + 1],
            )
        gain = resident.tile([P, PASSES * PACK], F32, name="gain")
        offset = resident.tile([P, PASSES * PACK], F32, name="offset")

        nc.scalar.activation(
            out=turns_flat,
            in_=phase_flat,
            func=ACT.Copy,
            scale=0.5 / math.pi,
            bias=ROUND_MAGIC,
        )
        nc.scalar.activation(out=turns_flat, in_=turns_flat, func=ACT.Copy, bias=-ROUND_MAGIC)

        def take_off_turns():
            nc.vector.scalar_tensor_tensor(
                out=phase_flat,
                in0=phase_flat,
                scalar=0.5 / math.pi,
                in1=turns_flat,
                op0=ALU.mult,
                op1=ALU.subtract,
            )

        def absolute_phase():
            nc.vector.scalar_tensor_tensor(
                out=turns_flat,
                in0=phase_flat,
                scalar=-1.0,
                in1=phase_flat,
                op0=ALU.mult,
                op1=ALU.max,
            )

        w_grouped = {}
        w_codes = {}
        w_scales = {}

        def grouped_piece(index):
            m, c, g = pieces[index]
            if (m, c) not in w_grouped:
                w_grouped[(m, c)] = resident.tile(
                    [P, PASSES, CHUNK, PACK], BF16, name="w_grouped%d_%d" % (m, c), align_bytes=64
                )
            return w_grouped[(m, c)][:, g]

        def regroup_weight_columns(copy, index, first, last):
            m, c, g = pieces[index]
            copy(
                out=grouped_piece(index)[:, first:last].rearrange("p (a i) t -> p a t i", i=RUN),
                in_=w_rows[(m, g)][:, :, c * CHUNK + first : c * CHUNK + last].rearrange(
                    "p t (a i) -> p a t i", i=RUN
                ),
            )

        def regroup_weight_piece(index):
            regroup_weight_columns(nc.scalar.copy, index, 0, CHUNK)

        def quantise_weight(m, c, first_pass, last_pass):
            if (m, c) not in w_codes:
                w_codes[(m, c)] = resident.tile(
                    [P, PASSES, CHUNK], U32, name="w_codes%d_%d" % (m, c), align_bytes=64
                )
                w_scales[(m, c)] = resident.tile(
                    [P, PASSES, CHUNK], U8, name="w_scales%d_%d" % (m, c), align_bytes=64
                )
            passes = slice(first_pass, last_pass + 1)
            nc.vector.quantize_mx(
                out=w_codes[(m, c)][:, passes].rearrange("p g n -> p (g n)").bitcast(FP8X4),
                scales=w_scales[(m, c)][:, passes].rearrange("p g n -> p (g n)"),
                in_=w_grouped[(m, c)][:, passes].rearrange("p g n t -> p (g n t)"),
            )

        stats = []
        mean_var = []
        rstd = []
        shift = []

        def measure(tt, part):
            if part == 0:
                stats.append(small.tile([P, D // BN_STATS_MAX, BN_STATS_DIM], F32, name="stats"))
            nc.vector.bn_stats(
                out=stats[tt][:, part, :],
                in_=x_tiles[tt][:, part * BN_STATS_MAX : (part + 1) * BN_STATS_MAX],
            )

        def aggregate(tt):
            mean_var.append(small.tile([P, 2], F32, name="mean_var"))
            nc.vector.bn_aggr(out=mean_var[tt][:], in_=stats[tt][:].rearrange("p a b -> p (a b)"))

        def scale(tt):
            var_eps = small.tile([P, 1], F32, name="var_eps")
            nc.vector.tensor_scalar_add(out=var_eps[:], in0=mean_var[tt][:, 1:2], scalar1=EPS)
            rstd.append(small.tile([P, 1], F32, name="rstd"))
            nc.gpsimd.tensor_tensor(out=rstd[tt][:], in0=var_eps[:], in1=minus_half[:], op=ALU.pow)

        def scale_and_shift(tt):
            scale(tt)
            minus_mean = small.tile([P, 1], F32, name="minus_mean")
            nc.vector.tensor_scalar_mul(out=minus_mean[:], in0=mean_var[tt][:, 0:1], scalar1=-1.0)
            shift.append(small.tile([P, 1], F32, name="shift"))
            nc.gpsimd.tensor_tensor(out=shift[tt][:], in0=minus_mean[:], in1=rstd[tt][:], op=ALU.mult)

        measure(0, 0)
        measure(0, 1)
        for tt in range(1, TOKEN_TILES):
            measure(tt, 0)
            aggregate(tt - 1)
            measure(tt, 1)
            if tt - 1 < SCALAR_TILES:
                scale_and_shift(tt - 1)
            else:
                scale(tt - 1)
        aggregate(TOKEN_TILES - 1)
        if FRAC_EARLY:
            take_off_turns()
        scale(TOKEN_TILES - 1)
        nc.gpsimd.tensor_copy(out=gain[:], in_=gain_bf[:].rearrange("p g t -> p (g t)"))
        nc.gpsimd.tensor_copy(out=offset[:], in_=offset_bf[:].rearrange("p g t -> p (g t)"))

        planes = resident.tile([P, PASSES, PACK, TOKENS], BF16, name="planes")
        x_grouped = resident.tile([P, PASSES, TOKENS, PACK], BF16, name="x_grouped", align_bytes=64)
        x_codes = resident.tile([P, PASSES, TOKENS], U32, name="x_codes", align_bytes=64)
        x_scales = resident.tile([P, PASSES, TOKENS], U8, name="x_scales", align_bytes=64)

        with tc.psum_pool(name="transposed", bufs=1) as transposed:
            z_t = {}
            for g in range(PASSES):
                for t in range(PACK):
                    z_t[(g, t)] = transposed.tile([P, TOKENS], F32, name="z_t%d_%d" % (g, t))
            z = [norm.tile([P, PASSES, PACK, P], F32, name="z") for tt in range(TOKEN_TILES)]

            def x_sorted(tt, g):
                return x_tiles[tt][:].rearrange("q (g c t) -> q g t c", g=PASSES, t=PACK)[:, g]

            def normalise_on_scalar(tt, g):
                nc.scalar.activation(
                    out=z[tt][:, g],
                    in_=x_sorted(tt, g),
                    func=ACT.Identity,
                    scale=rstd[tt][:, 0:1],
                    bias=shift[tt][:, 0:1],
                )

            def normalise_on_vector(tt, g):
                nc.vector.tensor_scalar(
                    out=z[tt][:, g],
                    in0=x_sorted(tt, g),
                    scalar1=mean_var[tt][:, 0:1],
                    scalar2=rstd[tt][:, 0:1],
                    op0=ALU.subtract,
                    op1=ALU.mult,
                )

            def transpose(tt, g):
                for t in range(PACK):
                    nc.tensor.transpose(
                        z_t[(g, t)][:, tt * P : (tt + 1) * P], z[tt][:, g, t, :], identity[:]
                    )

            for tt in range(SCALAR_TILES):
                for g in range(PASSES):
                    normalise_on_scalar(tt, g)
                    transpose(tt, g)
            regroup_weight_piece(0)
            for tt in range(SCALAR_TILES, TOKEN_TILES):
                for g in range(PASSES):
                    normalise_on_vector(tt, g)
                    transpose(tt, g)
            if not FRAC_EARLY:
                take_off_turns()

            for t in range(VECTOR_BANKS):
                nc.vector.tensor_scalar(
                    out=planes[:, 0, t, :],
                    in0=z_t[(0, t)][:],
                    scalar1=gain[:, t : t + 1],
                    scalar2=offset[:, t : t + 1],
                    op0=ALU.mult,
                    op1=ALU.add,
                )
            for g in range(PASSES):
                for t in range(VECTOR_BANKS if g == 0 else 0, PACK):
                    nc.scalar.activation(
                        out=planes[:, g, t, :],
                        in_=z_t[(g, t)][:],
                        func=ACT.Identity,
                        scale=gain[:, g * PACK + t : g * PACK + t + 1],
                        bias=offset[:, g * PACK + t : g * PACK + t + 1],
                    )

        def group_x(g):
            nc.vector.tensor_copy(
                out=x_grouped[:, g].rearrange("p (a i) t -> p a t i", i=RUN),
                in_=planes[:, g].rearrange("p t (a i) -> p a t i", i=RUN),
            )

        quantise_weight(0, 0, 0, 0)
        group_x(0)
        absolute_phase()
        regroup_weight_columns(nc.vector.tensor_copy, 2, 0, HALF)
        group_x(1)

        weight_banks = stack.enter_context(
            tc.psum_pool(name="weight_banks", bufs=2, reuse_waits="tile")
        )
        rope_banks = stack.enter_context(
            tc.psum_pool(name="rope_banks", bufs=LOOKAHEAD + 1, reuse_waits="tile")
        )
        plain_banks = stack.enter_context(
            tc.psum_pool(name="plain_banks", bufs=LOOKAHEAD + 1, reuse_waits="tile")
        )

        halves = TENSOR_HALVES
        half_banks = {}

        def regroup_half(number):
            index, half = halves[number]
            m, c, g = pieces[index]
            bank = weight_banks.tile([P, HALF * PACK], BF16, name="bank")
            for part in range(2):
                first = c * CHUNK + half * HALF + part * P
                nc.tensor.matmul(
                    out=bank[:, part * P * PACK : (part + 1) * P * PACK].rearrange(
                        "p (n t) -> p t n", t=PACK
                    ),
                    lhsT=identity_bf[:],
                    rhs=w_rows[(m, g)][:, :, first : first + P],
                    start=True,
                    stop=True,
                )
            half_banks[number] = bank

        def copy_half(number):
            index, half = halves[number]
            nc.scalar.copy(
                out=grouped_piece(index)[:, half * HALF : (half + 1) * HALF, :].rearrange(
                    "p n t -> p (n t)"
                ),
                in_=half_banks[number][:],
            )

        def copy_piece(index):
            for half in range(2):
                copy_half(halves.index((index, half)))

        regroup_half(0)
        regroup_half(1)
        copy_piece(1)
        for number in range(2, EARLY_HALVES):
            regroup_half(number)
        nc.scalar.activation(
            out=sin_table[:].rearrange("p b c -> p (b c)"), in_=phase_flat, func=ACT.Sin, scale=2.0 * math.pi
        )
        nc.scalar.activation(
            out=cos_table[:].rearrange("p b c -> p (b c)"),
            in_=turns_flat,
            func=ACT.Sin,
            scale=-2.0 * math.pi,
            bias=0.5 * math.pi,
        )
        def copy_two():
            if (2, 1) in halves:
                copy_half(halves.index((2, 1)))
            else:
                regroup_weight_columns(nc.scalar.copy, 2, HALF, CHUNK)

        if TWO_FIRST:
            copy_two()
        regroup_weight_piece(3)
        if not TWO_FIRST:
            copy_two()
        regroup_weight_columns(nc.scalar.copy, 5, GPSIMD_COLUMNS, CHUNK)

        quantise_weight(0, 0, 1, 1)
        for first in range(0, TOKENS, X_TOKENS):
            for g in range(PASSES):
                nc.vector.quantize_mx(
                    out=x_codes[:, g, first : first + X_TOKENS].bitcast(FP8X4),
                    scales=x_scales[:, g, first : first + X_TOKENS],
                    in_=x_grouped[:, g, first : first + X_TOKENS].rearrange("p r t -> p (r t)"),
                )

        if EARLY_TWO:
            quantise_weight(0, 1, 0, 0)

        fence = resident.tile([P, 1], U32, name="fence")
        last_codes = w_codes[(0, 1)][:, 0, CHUNK - 1 : CHUNK] if EARLY_TWO else x_codes[:, PASSES - 1, TOKENS - 1 : TOKENS]
        nc.gpsimd.tensor_copy(out=fence[:], in_=last_codes)

        if GPSIMD_COLUMNS:
            m, c, g = pieces[5]
            nc.gpsimd.tensor_scalar(
                out=grouped_piece(5)[:, 0:GPSIMD_COLUMNS],
                in0=w_rows[(m, g)][:, :, c * CHUNK : c * CHUNK + GPSIMD_COLUMNS].rearrange(
                    "p t n -> p n t"
                ),
                scalar1=1.0,
                scalar2=0.0,
                op0=ALU.mult,
                op1=ALU.add,
            )

        rope_jobs = [(m, c, tt) for m in (0, 1) for c in range(CHUNKS) for tt in range(TOKEN_TILES)]
        banks = {}

        def multiply(m, c, tt):
            if m == 2 and c * TOKEN_TILES + tt in (3, 4):
                acc = weight_banks.tile([P, CHUNK], F32, name="bank")
            else:
                pool = rope_banks if m < 2 else plain_banks
                acc = pool.tile([P, CHUNK], F32, name="acc")
            for g in range(PASSES):
                nc.tensor.matmul_mx(
                    out=acc[:],
                    lhsT=x_codes[:, g, tt * P : (tt + 1) * P].bitcast(FP8X4),
                    lhsT_scale=x_scales[:, g, tt * P : (tt + 1) * P],
                    rhs=w_codes[(m, c)][:, g, :].bitcast(FP8X4),
                    rhs_scale=w_scales[(m, c)][:, g, :],
                    start=(g == 0),
                    stop=(g == PASSES - 1),
                )
            banks[(m, c, tt)] = acc

        pairs = []

        def rope(step):
            m, c, tt = rope_jobs[step]
            part = step % 2
            if part == 0:
                straight = work.tile([P, 2, CHUNK], F32, name="straight")
                crossed = work.tile([P, 2, CHUNK], F32, name="crossed")
                turned = results.tile([P, 2, CHUNK], F32, name="turned")
                pairs.append((straight, crossed, turned))
            straight, crossed, turned = pairs[-1]
            acc = banks[(m, c, tt)]
            nc.vector.tensor_tensor(
                out=straight[:, part].rearrange("p (r m) -> p r m", m=ANGLES),
                in0=acc[:].rearrange("p (r m) -> p r m", m=ANGLES),
                in1=cos_table[:, tt, :].unsqueeze(1).to_broadcast([P, REPEATS, ANGLES]),
                op=ALU.mult,
            )
            nc.vector.tensor_tensor(
                out=crossed[:, part].rearrange("p (r i two) -> p r i two", r=REPEATS, two=2),
                in0=acc[:].rearrange("p (r i two) -> p r i two", r=REPEATS, two=2)[:, :, :, ::-1],
                in1=sin_table[:, tt, :]
                .rearrange("p (i two) -> p i two", two=2)
                .unsqueeze(1)
                .to_broadcast([P, REPEATS, ANGLES // 2, 2]),
                op=ALU.mult,
            )

        def add(adder, step, count=1, first=0, last=CHUNK):
            part = step % 2
            straight, crossed, turned = (
                tile[:, part : part + count, first:last].rearrange("p b n -> p (b n)")
                if count == 1 or last - first == CHUNK
                else tile[:, part : part + count, first:last]
                for tile in pairs[step // 2]
            )
            adder.tensor_tensor(out=turned, in0=straight, in1=crossed, op=ALU.add)
            for bank in range(step, step + count):
                m, c, tt = rope_jobs[bank]
                nc.sync.dma_start(
                    out=out_rows[m][
                        tt * P : (tt + 1) * P, c * CHUNK + first : c * CHUNK + last
                    ],
                    in_=pairs[bank // 2][2][:, bank % 2, first:last],
                )

        unstored = []

        def store_plain():
            while unstored:
                plain, c, tt = unstored.pop()
                nc.scalar.dma_start(
                    out=out_rows[2][tt * P : (tt + 1) * P, c * CHUNK : (c + 1) * CHUNK],
                    in_=plain[:],
                )

        def finish_plain(c, tt):
            plain = plain_results.tile([P, CHUNK], F32, name="plain")
            nc.scalar.copy(out=plain[:], in_=banks[(2, c, tt)][:])
            store_plain()
            unstored.append((plain, c, tt))

        quantised = 1
        multiplied = 0
        for step in range(len(rope_jobs)):
            while (
                multiplied < min(step + LOOKAHEAD + 1, len(rope_jobs))
                and rope_jobs[multiplied][:2] in chunks[:quantised]
            ):
                multiply(*rope_jobs[multiplied])
                multiplied += 1
            for number in HALVES_AFTER.get(step, ()):
                regroup_half(number)
            for c, tt in V_PRODUCTS.get(step, ()):
                multiply(2, c, tt)
            for work_item in SCALAR_WORK.get(step, ()):
                if isinstance(work_item, tuple):
                    finish_plain(*work_item)
                else:
                    if work_item in TENSOR_PIECES:
                        copy_piece(work_item)
                    else:
                        regroup_weight_columns(nc.scalar.copy, work_item, 0, HALF)
                        store_plain()
                        regroup_weight_columns(nc.scalar.copy, work_item, HALF, CHUNK)
                    store_plain()
            if step >= FLUSH_FROM:
                store_plain()
            rope(step)
            if step in VECTOR_ADDS and VADD_FIRST:
                add(nc.vector, VECTOR_ADDS[step])
            if step in QUANTISE_BEHIND:
                quantise_weight(
                    *chunks[quantised], 1 if quantised == 1 and EARLY_TWO else 0, PASSES - 1
                )
                quantised += 1
            if step in VECTOR_ADDS and not VADD_FIRST:
                add(nc.vector, VECTOR_ADDS[step])
            if step in VECTOR_ADDS.values():
                pass
            elif step < SINGLE_FROM:
                if step % 2 == 1:
                    add(nc.gpsimd, step - 1, count=2)
            elif step < LAST_GPSIMD:
                add(nc.gpsimd, step)
            elif step > LAST_GPSIMD and step < len(rope_jobs) - 1:
                add(nc.vector, step - 1)
            elif step == len(rope_jobs) - 1:
                add(nc.vector, step - 1)
                add(nc.vector, step, last=CHUNK // 2)
                add(nc.vector, step, first=CHUNK // 2)
        store_plain()
